import numpy as np
import ml_dtypes


def mxq(x, axis, fmt="e4m3"):
    dtype, down = {"e4m3": (ml_dtypes.float8_e4m3fn, 7), "e5m2": (ml_dtypes.float8_e5m2, 14)}[fmt]
    v = np.moveaxis(np.asarray(x, np.float32).astype(ml_dtypes.bfloat16).astype(np.float64), axis, -1)
    blocks = v.reshape(v.shape[:-1] + (-1, 32))
    amax = np.abs(blocks).max(-1, keepdims=True)
    byte = np.maximum(np.where(amax > 0, np.frexp(amax)[1] - 1 + 127, 0) - down, 1)
    scale = np.exp2(byte - 127.0)
    codes = (blocks / scale).astype(np.float32).astype(dtype).astype(np.float64)
    return np.moveaxis((codes * scale).reshape(v.shape), -1, axis)


WIDE = False


def mx_kscale(k):
    if not WIDE:
        return np.ones(k)
    levels = np.array([10, -10, 5, -5, 0])
    if k % 512:
        return np.exp2(np.random.permutation(np.resize(levels, k // 32))).repeat(32)
    a = np.empty((k // 512, 16))
    for p in range(k // 512):
        a[p, :8] = np.random.permutation(np.resize(levels, 8))
        for g in range(8):
            far = levels[np.abs(levels - a[p, g]) >= 10]
            a[p, g + 8] = far[np.random.randint(len(far))]
    return np.exp2(a.ravel()).repeat(32)


BF16 = ml_dtypes.bfloat16


def bf(x):
    return np.asarray(x, np.float32).astype(BF16)


def f64(x):
    return np.asarray(x).astype(np.float64)


B, DD, DK, CI, CO, L, NLC, PAD, KL = 1, 2, 2, 512, 128, 256, 4, 4, 9


def seg_lengths():
    cover = (L + PAD + PAD) // NLC - PAD - PAD
    lens = [cover] * NLC
    lens[-1] = L - cover * (NLC - 1)
    return lens


def setup_inputs():
    s = mx_kscale(CI)
    x = np.random.standard_normal((B, DD, DK, CI, L)) * s[:, None]
    weight = np.random.standard_normal((DD, DK, CO, CI, NLC, KL)) / np.sqrt(CI * KL) / s[:, None, None]
    bias = np.random.standard_normal((DD, DK, CO, NLC)) * 0.5
    return {"x": bf(x), "weight": bf(weight[..., None, :]), "conv_bias_param": bf(bias[..., None])}


def core(x, weight, conv_bias_param):
    xq = mxq(f64(x), 3, "e4m3")
    wq = mxq(f64(weight), 3, "e4m3")
    bias = f64(conv_bias_param)
    outs, start = [], 0
    for i, ln in enumerate(seg_lengths()):
        acc = np.zeros((B, DD, DK, CO, ln))
        for f in range(KL):
            lo = max(start, PAD - f)
            hi = min(start + ln, L + PAD - f)
            xs = xq[..., lo + f - PAD:hi + f - PAD].swapaxes(-1, -2)
            wf = wq[:, :, :, :, i, 0, f].swapaxes(-1, -2)
            acc[..., lo - start:hi - start] += (xs @ wf).swapaxes(-1, -2)
        outs.append(acc + bias[None, :, :, :, i, :])
        start += ln
    return np.concatenate(outs, axis=-1)


def e4m3fn_bytes(y):
    return np.clip(np.asarray(y, np.float64), -448.0, 448.0).astype(np.float32).astype(ml_dtypes.float8_e4m3fn).view(np.uint8)


def reference(x, weight, conv_bias_param):
    out = core(x, weight, conv_bias_param)
    s = np.max(np.abs(out)) / 448.0
    return out, e4m3fn_bytes(out / s)

@@ -1,0 +1,217 @@
+from contextlib import ExitStack
+
+import concourse.mybir as mybir
+from concourse.masks import make_identity
+
+F32 = mybir.dt.float32
+BF16 = mybir.dt.bfloat16
+I32 = mybir.dt.int32
+U8 = mybir.dt.uint8
+FP8 = mybir.dt.float8_e4m3fn
+FP8X4 = mybir.dt.float8_e4m3fn_x4
+ACT = mybir.ActivationFunctionType
+ALU = mybir.AluOpType
+AX = mybir.AxisListType
+
+G, CO, CI, SF, L, KL = 4, 128, 512, 36, 256, 9
+P = 128
+SEG_START = (0, 58, 116, 174)
+SEG_END = (58, 116, 174, 256)
+SEG_BASE = (0, 0, 64, 128)
+CHUNK = 4
+NCHUNK = SF // CHUNK
+NBANK = 2 * G * NCHUNK
+BLOCKS = (4,) * 16 + (2, 2, 2, 1, 1)
+MAX_POP = 3
+
+FLOPS = 2 * G * CO * CI * KL * L
+
+
+def tile_partiallyunsharedconv1d_pa_kernel(tc, x, weight, conv_bias_param, out_0, out_1):
+    nc = tc.nc
+    w4 = weight.rearrange("d k o c s x f -> (d k) o (c s x f)")
+    x4 = x.rearrange("o d k c l -> (o d k) c l").rearrange("g (a v) l -> g a (v l)", v=2)
+    xv = x4.rearrange("g (b u q) y -> b u q g y", b=16, u=2, q=8)
+    bias_v = conv_bias_param.rearrange("d k o s x -> o (d k) (s x)")
+    out0_v = out_0.rearrange("o d k c l -> (o d k) c l")
+    out1_v = out_1.rearrange("o d k c l -> c (o d k) l")
+
+    with ExitStack() as ctx:
+        const = ctx.enter_context(tc.tile_pool(name="const", bufs=1))
+        rawp = ctx.enter_context(tc.tile_pool(name="rawp", bufs=5))
+        grp = ctx.enter_context(tc.tile_pool(name="grp", bufs=12))
+        wqp = ctx.enter_context(tc.tile_pool(name="wqp", bufs=10))
+        pst = ctx.enter_context(tc.psum_pool(name="pst", bufs=6))
+        psa = ctx.enter_context(tc.psum_pool(name="psa", bufs=2))
+
+        bias_b = const.tile([P, G, 4], BF16)
+        nc.scalar.dma_start(out=bias_b[:], in_=bias_v)
+        raw_x = const.tile([P, G, 2, 2 * L], BF16)
+        for q in range(8):
+            for u in range(2):
+                nc.scalar.dma_start(out=raw_x[q:P:8, :, u, :], in_=xv[:, u, q, :, :])
+
+        raws = {}
+
+        def load_unit(unit):
+            g, h = divmod(unit, 2)
+            raw = rawp.tile([P, 16 * 576], BF16, tag="raw")
+            src = w4[g, 64 * h:64 * h + 64, :].rearrange("c (b u y) -> c b u y", b=16, u=2)
+            for u in range(2):
+                nc.sync.dma_start(
+                    out=raw[u:P:2, :].rearrange("c (b y) -> c b y", b=16),
+                    in_=src[:, :, u, :],
+                )
+            raws[unit] = raw
+
+        for unit in range(5):
+            load_unit(unit)
+
+        ident_b = const.tile([P, P], BF16)
+        make_identity(nc, ident_b[:])
+        ident_f = const.tile([P, P], F32)
+        make_identity(nc, ident_f[:])
+        zero = const.tile([P, 1], F32)
+        nc.vector.memset(zero[:], 0.0)
+        bias_f = const.tile([P, G * 4], F32)
+        nc.vector.tensor_copy(out=bias_f[:], in_=bias_b[:].rearrange("p g s -> p (g s)"))
+
+        xc = const.tile([P, KL, G, L], I32, align_bytes=64)
+        xs = const.tile([P, KL, G, L], U8, align_bytes=64)
+        xg = const.tile([P, G, 4 * L], BF16, align_bytes=64)
+        xc_fg = xc[:].rearrange("p f g j -> p (f g) j")
+        nc.vector.memset(xc_fg[:, :, 0:4], 0)
+        nc.vector.memset(xc_fg[:, :, L - 4:L], 0)
+        nc.vector.memset(xs[:].rearrange("p f g j -> p (f g j)").bitcast(I32), 0)
+        for g in range(G):
+            dst = xg[:, g, :].rearrange("p (l v u) -> p l v u", v=2, u=2)
+            src = raw_x[:, g, :, :].rearrange("p u (v l) -> p l v u", v=2)
+            if g < 2:
+                nc.vector.tensor_copy(out=dst, in_=src)
+            else:
+                nc.scalar.copy(out=dst, in_=src)
+        for g in range(G):
+            nc.vector.quantize_mx(out=xc[:, 4, g, :].bitcast(FP8X4), scales=xs[:, 4, g, :], in_=xg[:, g, :])
+
+        def shift_copies(g0, g1):
+            for f in range(KL):
+                d = f - 4
+                if d == 0:
+                    continue
+                lo, hi = max(0, -d), L - max(0, d)
+                nc.vector.tensor_copy(out=xc[:, f, g0:g1, lo:hi], in_=xc[:, 4, g0:g1, lo + d:hi + d])
+                nc.vector.tensor_copy(out=xs[:, f, g0:g1, lo:hi], in_=xs[:, 4, g0:g1, lo + d:hi + d])
+
+        shift_copies(0, 1)
+        shift_copies(1, G)
+
+        o_sb = const.tile([P, G, L], F32)
+        o8 = const.tile([P, G, L], FP8)
+        stat = const.tile([P, G], F32)
+        grs = {}
+        accs = {}
+
+        def transposes(j):
+            unit, c = divmod(j, NCHUNK)
+            raw = raws[unit]
+            tp = pst.tile([P, 2 * CHUNK, P], BF16, tag="tp")
+            for i in range(CHUNK):
+                for v in range(2):
+                    first = v * SF + CHUNK * c + i
+                    nc.tensor.transpose(tp[:, 2 * i + v, :], raw[:, first:first + 72 * 127 + 1:72], ident_b[:])
+            return tp
+
+        def evacuate(j, tp):
+            unit, c = divmod(j, NCHUNK)
+            g, h = divmod(unit, 2)
+            if h == 0:
+                gr = grp.tile([P, CHUNK * CO * 4], BF16, tag="gr", align_bytes=64)
+                grs[(g, c)] = gr
+            gr = grs[(g, c)]
+            dst = gr[:].bitcast(F32).rearrange("p (i o v) -> p i o v", i=CHUNK, v=2)[:, :, 64 * h:64 * h + 64, :]
+            src = tp[:].rearrange("p a n -> p (a n)").bitcast(F32).rearrange("p (i v c) -> p i c v", i=CHUNK, v=2)
+            if j % 6 == 5 and j >= 12:
+                nc.vector.tensor_copy(out=dst, in_=src)
+            else:
+                nc.scalar.copy(out=dst, in_=src)
+
+        def quantize(g, c):
+            wq = wqp.tile([P, CHUNK * CO], I32, tag="wq", align_bytes=64)
+            ws = wqp.tile([P, CHUNK * CO], U8, tag="ws", align_bytes=64)
+            nc.vector.quantize_mx(out=wq[:].bitcast(FP8X4), scales=ws[:], in_=grs[(g, c)][:])
+            return (g, c, wq, ws)
+
+        def finish_segment(g, s):
+            acc = accs[g]
+            a, st, en = SEG_BASE[s], SEG_START[s], SEG_END[s]
+            nc.scalar.activation(
+                out=o_sb[:, g, st:en], in_=acc[:, s, st - a:en - a], func=ACT.Identity,
+                bias=bias_f[:, 4 * g + s:4 * g + s + 1], scale=1.0,
+            )
+            if s == 3:
+                nc.scalar.dma_start(out=out0_v[g], in_=o_sb[:, g, :])
+                nc.vector.tensor_reduce(out=stat[:, g:g + 1], in_=o_sb[:, g, :], axis=AX.X, op=ALU.max,
+                                        apply_absolute_value=True)
+
+        def multiply(item):
+            g, c, wq, ws = item
+            if c == 0:
+                acc = psa.tile([P, 4, P], F32, tag="acc")
+                accs[g] = acc
+            acc = accs[g]
+            for i in range(CHUNK):
+                s, f = divmod(CHUNK * c + i, KL)
+                a = SEG_BASE[s]
+                nc.tensor.matmul_mx(
+                    out=acc[:, s, :],
+                    lhsT=wq[:, CO * i:CO * (i + 1)].bitcast(FP8X4), lhsT_scale=ws[:, CO * i:CO * (i + 1)],
+                    rhs=xc[:, f, g, a:a + P].bitcast(FP8X4), rhs_scale=xs[:, f, g, a:a + P],
+                    start=(f == 0), stop=(f == KL - 1),
+                )
+                if f == KL - 1:
+                    finish_segment(g, s)
+
+        with tc.manual_schedule(engines={mybir.EngineType.PE}):
+            ready = []
+            j0 = 0
+            next_unit = 5
+            for blk in BLOCKS:
+                banks = list(range(j0, j0 + blk))
+                j0 += blk
+                tps = []
+                for j in banks:
+                    tps.append(transposes(j))
+                last_unit = banks[0] >= NBANK - NCHUNK
+                pops = len(ready) if last_unit else min(len(ready), MAX_POP)
+                for item in ready[:pops]:
+                    multiply(item)
+                ready = ready[pops:]
+                for j, tp in zip(banks, tps):
+                    evacuate(j, tp)
+                    unit, c = divmod(j, NCHUNK)
+                    if unit % 2 == 1:
+                        ready.append(quantize(unit // 2, c))
+                    if c == NCHUNK - 1 and next_unit < 2 * G:
+                        load_unit(next_unit)
+                        next_unit += 1
+            for item in ready:
+                multiply(item)
+
+        m1 = const.tile([P, 1], F32)
+        nc.vector.tensor_reduce(out=m1[:], in_=stat[:], axis=AX.X, op=ALU.max)
+        spread = pst.tile([P, P], F32, tag="tp")
+        nc.tensor.transpose(spread[:], m1[:, 0:1].to_broadcast([P, P]), ident_f[:])
+        amax = const.tile([P, 1], F32)
+        nc.vector.tensor_reduce(out=amax[:], in_=spread[:], axis=AX.X, op=ALU.max)
+        rec = const.tile([P, 1], F32)
+        nc.vector.reciprocal(out=rec[:], in_=amax[:])
+        fac = const.tile([P, 1], F32)
+        nc.vector.tensor_scalar(out=fac[:], in0=rec[:], scalar1=448.0, scalar2=None, op0=ALU.mult)
+        nc.scalar.activation(out=o8[:, 3, :], in_=o_sb[:, 3, :], func=ACT.Identity, scale=fac[:, 0:1],
+                             bias=zero[:, 0:1], saturate=False)
+        nc.vector.tensor_scalar(out=o8[:, 0:2, :], in0=o_sb[:, 0:2, :], scalar1=fac[:, 0:1], scalar2=None,
+                                op0=ALU.mult, saturate=False)
+        nc.sync.dma_start(out=out1_v[:, 0:2, :], in_=o8[:, 0:2, :].bitcast(U8))
+        nc.vector.tensor_scalar(out=o8[:, 2, :], in0=o_sb[:, 2, :], scalar1=fac[:, 0:1], scalar2=None,
+                                op0=ALU.mult, saturate=False)
+        nc.sync.dma_start(out=out1_v[:, 2:4, :], in_=o8[:, 2:4, :].bitcast(U8))

@@ -20,9 +20,10 @@ SEG_END = (58, 116, 174, 256)
 SEG_BASE = (0, 0, 64, 128)
 CHUNK = 4
 NCHUNK = SF // CHUNK
-NBANK = 2 * G * NCHUNK
-BLOCKS = (4,) * 16 + (2, 2, 2, 1, 1)
-MAX_POP = 3
+NCO = 16
+NLOAD = CO // NCO
+V_CO = 8
+AHEAD = 6
 
 FLOPS = 2 * G * CO * CI * KL * L
 
@@ -30,45 +31,35 @@ FLOPS = 2 * G * CO * CI * KL * L
 def tile_partiallyunsharedconv1d_pa_kernel(tc, x, weight, conv_bias_param, out_0, out_1):
     nc = tc.nc
     w4 = weight.rearrange("d k o c s x f -> (d k) o (c s x f)")
-    x4 = x.rearrange("o d k c l -> (o d k) c l").rearrange("g (a v) l -> g a (v l)", v=2)
-    xv = x4.rearrange("g (b u q) y -> b u q g y", b=16, u=2, q=8)
+    xv = x.rearrange("o d k c l -> (o d k) c l").rearrange("g (p j) l -> p g (j l)", j=4)
     bias_v = conv_bias_param.rearrange("d k o s x -> o (d k) (s x)")
     out0_v = out_0.rearrange("o d k c l -> (o d k) c l")
     out1_v = out_1.rearrange("o d k c l -> c (o d k) l")
 
     with ExitStack() as ctx:
         const = ctx.enter_context(tc.tile_pool(name="const", bufs=1))
-        rawp = ctx.enter_context(tc.tile_pool(name="rawp", bufs=5))
-        grp = ctx.enter_context(tc.tile_pool(name="grp", bufs=12))
-        wqp = ctx.enter_context(tc.tile_pool(name="wqp", bufs=10))
-        pst = ctx.enter_context(tc.psum_pool(name="pst", bufs=6))
+        rawp = ctx.enter_context(tc.tile_pool(name="rawp", bufs=AHEAD + 2))
+        grp = ctx.enter_context(tc.tile_pool(name="grp", bufs=2))
+        wqp = ctx.enter_context(tc.tile_pool(name="wqp", bufs=12))
+        pst = ctx.enter_context(tc.psum_pool(name="pst", bufs=1))
         psa = ctx.enter_context(tc.psum_pool(name="psa", bufs=2))
 
+        raw_x = const.tile([P, G, 4 * L], BF16)
+        nc.sync.dma_start(out=raw_x[:], in_=xv)
         bias_b = const.tile([P, G, 4], BF16)
         nc.scalar.dma_start(out=bias_b[:], in_=bias_v)
-        raw_x = const.tile([P, G, 2, 2 * L], BF16)
-        for q in range(8):
-            for u in range(2):
-                nc.scalar.dma_start(out=raw_x[q:P:8, :, u, :], in_=xv[:, u, q, :, :])
 
         raws = {}
 
-        def load_unit(unit):
-            g, h = divmod(unit, 2)
-            raw = rawp.tile([P, 16 * 576], BF16, tag="raw")
-            src = w4[g, 64 * h:64 * h + 64, :].rearrange("c (b u y) -> c b u y", b=16, u=2)
-            for u in range(2):
-                nc.sync.dma_start(
-                    out=raw[u:P:2, :].rearrange("c (b y) -> c b y", b=16),
-                    in_=src[:, :, u, :],
-                )
-            raws[unit] = raw
+        def load(k):
+            g, n = divmod(k, NLOAD)
+            raw = rawp.tile([P, NCO, 4 * SF], BF16, tag="raw")
+            nc.sync.dma_start(out=raw[:], in_=w4[g, NCO * n:NCO * (n + 1), :].rearrange("c (p y) -> p c y", p=P))
+            raws[k] = raw
 
-        for unit in range(5):
-            load_unit(unit)
+        for k in range(AHEAD):
+            load(k)
 
-        ident_b = const.tile([P, P], BF16)
-        make_identity(nc, ident_b[:])
         ident_f = const.tile([P, P], F32)
         make_identity(nc, ident_f[:])
         zero = const.tile([P, 1], F32)
@@ -84,8 +75,8 @@ def tile_partiallyunsharedconv1d_pa_kernel(tc, x, weight, conv_bias_param, out_0
         nc.vector.memset(xc_fg[:, :, L - 4:L], 0)
         nc.vector.memset(xs[:].rearrange("p f g j -> p (f g j)").bitcast(I32), 0)
         for g in range(G):
-            dst = xg[:, g, :].rearrange("p (l v u) -> p l v u", v=2, u=2)
-            src = raw_x[:, g, :, :].rearrange("p u (v l) -> p l v u", v=2)
+            dst = xg[:, g, :].rearrange("p (l j) -> p l j", j=4)
+            src = raw_x[:, g, :].rearrange("p (j l) -> p l j", j=4)
             if g < 2:
                 nc.vector.tensor_copy(out=dst, in_=src)
             else:
@@ -102,8 +93,7 @@ def tile_partiallyunsharedconv1d_pa_kernel(tc, x, weight, conv_bias_param, out_0
                 nc.vector.tensor_copy(out=xc[:, f, g0:g1, lo:hi], in_=xc[:, 4, g0:g1, lo + d:hi + d])
                 nc.vector.tensor_copy(out=xs[:, f, g0:g1, lo:hi], in_=xs[:, 4, g0:g1, lo + d:hi + d])
 
-        shift_copies(0, 1)
-        shift_copies(1, G)
+        shift_copies(0, G)
 
         o_sb = const.tile([P, G, L], F32)
         o8 = const.tile([P, G, L], FP8)
@@ -111,35 +101,16 @@ def tile_partiallyunsharedconv1d_pa_kernel(tc, x, weight, conv_bias_param, out_0
         grs = {}
         accs = {}
 
-        def transposes(j):
-            unit, c = divmod(j, NCHUNK)
-            raw = raws[unit]
-            tp = pst.tile([P, 2 * CHUNK, P], BF16, tag="tp")
-            for i in range(CHUNK):
-                for v in range(2):
-                    first = v * SF + CHUNK * c + i
-                    nc.tensor.transpose(tp[:, 2 * i + v, :], raw[:, first:first + 72 * 127 + 1:72], ident_b[:])
-            return tp
-
-        def evacuate(j, tp):
-            unit, c = divmod(j, NCHUNK)
-            g, h = divmod(unit, 2)
-            if h == 0:
-                gr = grp.tile([P, CHUNK * CO * 4], BF16, tag="gr", align_bytes=64)
-                grs[(g, c)] = gr
-            gr = grs[(g, c)]
-            dst = gr[:].bitcast(F32).rearrange("p (i o v) -> p i o v", i=CHUNK, v=2)[:, :, 64 * h:64 * h + 64, :]
-            src = tp[:].rearrange("p a n -> p (a n)").bitcast(F32).rearrange("p (i v c) -> p i c v", i=CHUNK, v=2)
-            if j % 6 == 5 and j >= 12:
-                nc.vector.tensor_copy(out=dst, in_=src)
-            else:
-                nc.scalar.copy(out=dst, in_=src)
-
-        def quantize(g, c):
-            wq = wqp.tile([P, CHUNK * CO], I32, tag="wq", align_bytes=64)
-            ws = wqp.tile([P, CHUNK * CO], U8, tag="ws", align_bytes=64)
-            nc.vector.quantize_mx(out=wq[:].bitcast(FP8X4), scales=ws[:], in_=grs[(g, c)][:])
-            return (g, c, wq, ws)
+        def interleave(k):
+            g, n = divmod(k, NLOAD)
+            if n == 0:
+                gr = grp.tile([P, SF * CO * 4], BF16, tag="gr", align_bytes=64)
+                grs[g] = gr
+            dst = grs[g][:].rearrange("p (s o j) -> p o s j", s=SF, j=4)
+            src = raws[k][:].rearrange("p c (j s) -> p c s j", j=4)
+            c0 = NCO * n
+            nc.vector.tensor_copy(out=dst[:, c0:c0 + V_CO, :, :], in_=src[:, 0:V_CO, :, :])
+            nc.scalar.copy(out=dst[:, c0 + V_CO:c0 + NCO, :, :], in_=src[:, V_CO:NCO, :, :])
 
         def finish_segment(g, s):
             acc = accs[g]
@@ -153,8 +124,11 @@ def tile_partiallyunsharedconv1d_pa_kernel(tc, x, weight, conv_bias_param, out_0
                 nc.vector.tensor_reduce(out=stat[:, g:g + 1], in_=o_sb[:, g, :], axis=AX.X, op=ALU.max,
                                         apply_absolute_value=True)
 
-        def multiply(item):
-            g, c, wq, ws = item
+        def quantize_multiply(g, c):
+            wq = wqp.tile([P, CHUNK * CO], I32, tag="wq", align_bytes=64)
+            ws = wqp.tile([P, CHUNK * CO], U8, tag="ws", align_bytes=64)
+            w = CHUNK * CO * 4
+            nc.vector.quantize_mx(out=wq[:].bitcast(FP8X4), scales=ws[:], in_=grs[g][:, w * c:w * (c + 1)])
             if c == 0:
                 acc = psa.tile([P, 4, P], F32, tag="acc")
                 accs[g] = acc
@@ -171,31 +145,18 @@ def tile_partiallyunsharedconv1d_pa_kernel(tc, x, weight, conv_bias_param, out_0
                 if f == KL - 1:
                     finish_segment(g, s)
 
-        with tc.manual_schedule(engines={mybir.EngineType.PE}):
-            ready = []
-            j0 = 0
-            next_unit = 5
-            for blk in BLOCKS:
-                banks = list(range(j0, j0 + blk))
-                j0 += blk
-                tps = []
-                for j in banks:
-                    tps.append(transposes(j))
-                last_unit = banks[0] >= NBANK - NCHUNK
-                pops = len(ready) if last_unit else min(len(ready), MAX_POP)
-                for item in ready[:pops]:
-                    multiply(item)
-                ready = ready[pops:]
-                for j, tp in zip(banks, tps):
-                    evacuate(j, tp)
-                    unit, c = divmod(j, NCHUNK)
-                    if unit % 2 == 1:
-                        ready.append(quantize(unit // 2, c))
-                    if c == NCHUNK - 1 and next_unit < 2 * G:
-                        load_unit(next_unit)
-                        next_unit += 1
-            for item in ready:
-                multiply(item)
+        todo = []
+        for k in range(G * NLOAD):
+            if k + AHEAD < G * NLOAD:
+                load(k + AHEAD)
+            interleave(k)
+            for item in todo[:2]:
+                quantize_multiply(item[0], item[1])
+            todo = todo[2:]
+            if k % NLOAD == NLOAD - 1:
+                todo = [(k // NLOAD, c) for c in range(NCHUNK)]
+        for item in todo:
+            quantize_multiply(item[0], item[1])
 
         m1 = const.tile([P, 1], F32)
         nc.vector.tensor_reduce(out=m1[:], in_=stat[:], axis=AX.X, op=ALU.max)

@@ -22,8 +22,14 @@ CHUNK = 4
 NCHUNK = SF // CHUNK
 NCO = 16
 NLOAD = CO // NCO
-V_CO = 8
-AHEAD = 6
+AHEAD = 5
+V_CO = 14
+V_SHARE = {(3, 7): 10}
+BLOCK = 4
+P_AFTER = {0: 2, 1: 2, 2: 2, 3: 0, 4: 1, 5: 1, 6: 3, 7: 2, 8: 2}
+NW = SF // 2
+ROW_SLICES = 4
+V_BANKS = ()
 
 FLOPS = 2 * G * CO * CI * KL * L
 
@@ -38,27 +44,50 @@ def tile_partiallyunsharedconv1d_pa_kernel(tc, x, weight, conv_bias_param, out_0
 
     with ExitStack() as ctx:
         const = ctx.enter_context(tc.tile_pool(name="const", bufs=1))
-        rawp = ctx.enter_context(tc.tile_pool(name="rawp", bufs=AHEAD + 2))
-        grp = ctx.enter_context(tc.tile_pool(name="grp", bufs=2))
-        wqp = ctx.enter_context(tc.tile_pool(name="wqp", bufs=12))
-        pst = ctx.enter_context(tc.psum_pool(name="pst", bufs=1))
+        rowp = ctx.enter_context(tc.tile_pool(name="rowp", bufs=2))
+        rawp = ctx.enter_context(tc.tile_pool(name="rawp", bufs=AHEAD + 1))
+        grp = ctx.enter_context(tc.tile_pool(name="grp", bufs=1))
+        gcp = ctx.enter_context(tc.tile_pool(name="gcp", bufs=4))
+        wqp = ctx.enter_context(tc.tile_pool(name="wqp", bufs=10))
+        pst = ctx.enter_context(tc.psum_pool(name="pst", bufs=6))
         psa = ctx.enter_context(tc.psum_pool(name="psa", bufs=2))
 
-        raw_x = const.tile([P, G, 4 * L], BF16)
-        nc.sync.dma_start(out=raw_x[:], in_=xv)
+        stage = grp.tile([P, 2, G, 4 * L], BF16, tag="gr", align_bytes=64)
+        raw_x = stage[:, 0, :, :]
+        xg = stage[:, 1, :, :]
+        nc.sync.dma_start(out=raw_x, in_=xv)
         bias_b = const.tile([P, G, 4], BF16)
         nc.scalar.dma_start(out=bias_b[:], in_=bias_v)
 
+        rows = {}
         raws = {}
 
-        def load(k):
-            g, n = divmod(k, NLOAD)
+        def load_rows(g):
+            row = rowp.tile([P, CI * SF], BF16, tag="row")
+            w = CI * SF // ROW_SLICES
+            for i in range(ROW_SLICES):
+                nc.sync.dma_start(out=row[:, w * i:w * (i + 1)], in_=w4[g, :, w * i:w * (i + 1)])
+            rows[g] = row
+
+        def load(g, n):
             raw = rawp.tile([P, NCO, 4 * SF], BF16, tag="raw")
             nc.sync.dma_start(out=raw[:], in_=w4[g, NCO * n:NCO * (n + 1), :].rearrange("c (p y) -> p c y", p=P))
-            raws[k] = raw
+            raws[(g, n)] = raw
 
-        for k in range(AHEAD):
-            load(k)
+        order = [(0, -1)] + [(1, n) for n in range(6)] + [(2, -1), (1, 6), (1, 7)] + [(3, n) for n in range(NLOAD)]
+        chunks = [item for item in order if item[1] >= 0]
+        issued = []
+
+        def issue_until(item):
+            while item not in issued:
+                nxt = order[len(issued)]
+                if nxt[1] < 0:
+                    load_rows(nxt[0])
+                else:
+                    load(nxt[0], nxt[1])
+                issued.append(nxt)
+
+        issue_until(chunks[AHEAD - 1])
 
         ident_f = const.tile([P, P], F32)
         make_identity(nc, ident_f[:])
@@ -69,31 +98,34 @@ def tile_partiallyunsharedconv1d_pa_kernel(tc, x, weight, conv_bias_param, out_0
 
         xc = const.tile([P, KL, G, L], I32, align_bytes=64)
         xs = const.tile([P, KL, G, L], U8, align_bytes=64)
-        xg = const.tile([P, G, 4 * L], BF16, align_bytes=64)
         xc_fg = xc[:].rearrange("p f g j -> p (f g) j")
         nc.vector.memset(xc_fg[:, :, 0:4], 0)
         nc.vector.memset(xc_fg[:, :, L - 4:L], 0)
-        nc.vector.memset(xs[:].rearrange("p f g j -> p (f g j)").bitcast(I32), 0)
+        xs_w = xs[:].rearrange("p f g j -> p (f g) j").bitcast(I32)
+        nc.vector.memset(xs_w[:, :, 0:1], 0)
+        nc.vector.memset(xs_w[:, :, L // 4 - 1:L // 4], 0)
+        nc.vector.memset(xs[:, 4, :, :].bitcast(I32), 0)
         for g in range(G):
             dst = xg[:, g, :].rearrange("p (l j) -> p l j", j=4)
             src = raw_x[:, g, :].rearrange("p (j l) -> p l j", j=4)
-            if g < 2:
-                nc.vector.tensor_copy(out=dst, in_=src)
-            else:
-                nc.scalar.copy(out=dst, in_=src)
+            nc.scalar.copy(out=dst, in_=src)
         for g in range(G):
             nc.vector.quantize_mx(out=xc[:, 4, g, :].bitcast(FP8X4), scales=xs[:, 4, g, :], in_=xg[:, g, :])
+        for f in range(KL):
+            d = f - 4
+            if d == 0:
+                continue
+            lo, hi = max(0, -d), L - max(0, d)
+            nc.vector.tensor_copy(out=xc[:, f, :, lo:hi], in_=xc[:, 4, :, lo + d:hi + d])
 
-        def shift_copies(g0, g1):
-            for f in range(KL):
-                d = f - 4
-                if d == 0:
-                    continue
-                lo, hi = max(0, -d), L - max(0, d)
-                nc.vector.tensor_copy(out=xc[:, f, g0:g1, lo:hi], in_=xc[:, 4, g0:g1, lo + d:hi + d])
-                nc.vector.tensor_copy(out=xs[:, f, g0:g1, lo:hi], in_=xs[:, 4, g0:g1, lo + d:hi + d])
-
-        shift_copies(0, G)
+        nw = L // 4
+        for d in (1, 2, 3):
+            nc.vector.tensor_copy(out=xs[:, 4 + d, :, 0:L - d], in_=xs[:, 4, :, d:L])
+        nc.vector.tensor_copy(out=xs[:, 8, :, :].bitcast(I32)[:, :, 0:nw - 1], in_=xs[:, 4, :, :].bitcast(I32)[:, :, 1:nw])
+        nc.vector.tensor_copy(out=xs[:, 0, :, :].bitcast(I32)[:, :, 1:nw], in_=xs[:, 4, :, :].bitcast(I32)[:, :, 0:nw - 1])
+        for d in (1, 2, 3):
+            nc.vector.tensor_copy(out=xs[:, d, :, :].bitcast(I32)[:, :, 1:nw], in_=xs[:, 4 + d, :, :].bitcast(I32)[:, :, 0:nw - 1])
+            nc.vector.tensor_copy(out=xs[:, d, :, 4 - d:4], in_=xs[:, 4, :, 0:d])
 
         o_sb = const.tile([P, G, L], F32)
         o8 = const.tile([P, G, L], FP8)
@@ -101,16 +133,20 @@ def tile_partiallyunsharedconv1d_pa_kernel(tc, x, weight, conv_bias_param, out_0
         grs = {}
         accs = {}
 
-        def interleave(k):
-            g, n = divmod(k, NLOAD)
+        def interleave(g, n):
             if n == 0:
                 gr = grp.tile([P, SF * CO * 4], BF16, tag="gr", align_bytes=64)
                 grs[g] = gr
             dst = grs[g][:].rearrange("p (s o j) -> p o s j", s=SF, j=4)
-            src = raws[k][:].rearrange("p c (j s) -> p c s j", j=4)
+            src = raws[(g, n)][:].rearrange("p c (j s) -> p c s j", j=4)
             c0 = NCO * n
-            nc.vector.tensor_copy(out=dst[:, c0:c0 + V_CO, :, :], in_=src[:, 0:V_CO, :, :])
-            nc.scalar.copy(out=dst[:, c0 + V_CO:c0 + NCO, :, :], in_=src[:, V_CO:NCO, :, :])
+            v = V_SHARE.get((g, n), V_CO)
+            if v > 0:
+                nc.vector.tensor_copy(out=dst[:, c0:c0 + v, :, :], in_=src[:, 0:v, :, :])
+            if v < NCO:
+                nc.scalar.copy(out=dst[:, c0 + v:c0 + NCO, :, :], in_=src[:, v:NCO, :, :])
+            pos = chunks.index((g, n)) + AHEAD
+            issue_until(chunks[min(pos, len(chunks) - 1)])
 
         def finish_segment(g, s):
             acc = accs[g]
@@ -124,11 +160,14 @@ def tile_partiallyunsharedconv1d_pa_kernel(tc, x, weight, conv_bias_param, out_0
                 nc.vector.tensor_reduce(out=stat[:, g:g + 1], in_=o_sb[:, g, :], axis=AX.X, op=ALU.max,
                                         apply_absolute_value=True)
 
-        def quantize_multiply(g, c):
+        def quantize(g, c, grouped):
             wq = wqp.tile([P, CHUNK * CO], I32, tag="wq", align_bytes=64)
             ws = wqp.tile([P, CHUNK * CO], U8, tag="ws", align_bytes=64)
-            w = CHUNK * CO * 4
-            nc.vector.quantize_mx(out=wq[:].bitcast(FP8X4), scales=ws[:], in_=grs[g][:, w * c:w * (c + 1)])
+            nc.vector.quantize_mx(out=wq[:].bitcast(FP8X4), scales=ws[:], in_=grouped)
+            return (g, c, wq, ws)
+
+        def multiply(item):
+            g, c, wq, ws = item
             if c == 0:
                 acc = psa.tile([P, 4, P], F32, tag="acc")
                 accs[g] = acc
@@ -145,18 +184,63 @@ def tile_partiallyunsharedconv1d_pa_kernel(tc, x, weight, conv_bias_param, out_0
                 if f == KL - 1:
                     finish_segment(g, s)
 
-        todo = []
-        for k in range(G * NLOAD):
-            if k + AHEAD < G * NLOAD:
-                load(k + AHEAD)
-            interleave(k)
-            for item in todo[:2]:
-                quantize_multiply(item[0], item[1])
-            todo = todo[2:]
-            if k % NLOAD == NLOAD - 1:
-                todo = [(k // NLOAD, c) for c in range(NCHUNK)]
-        for item in todo:
-            quantize_multiply(item[0], item[1])
+        WIDE = CHUNK * CO * 4
+        gcs = {}
+
+        def turn(g, w):
+            words = rows[g][:].bitcast(F32)
+            tp = pst.tile([P, 4, P], F32, tag="tp")
+            for t in range(4):
+                first = t * NW + w
+                nc.tensor.transpose(tp[:, t, :], words[:, first:first + 4 * NW * 127 + 1:4 * NW], ident_f[:])
+            return tp
+
+        def empty(g, w, tp):
+            if w % 2 == 0:
+                gc = gcp.tile([P, WIDE], BF16, tag="gc", align_bytes=64)
+                gcs[g] = gc
+            gc = gcs[g]
+            half = WIDE // 2
+            dst = gc[:, half * (w % 2):half * (w % 2 + 1)].rearrange("p (e o t) -> p e o t", e=2, t=4)
+            src = tp[:].rearrange("p t o -> p (t o)").bitcast(BF16).rearrange("p (t o e) -> p e o t", t=4, e=2)
+            nc.scalar.copy(out=dst, in_=src)
+
+        banks = [(0, w) for w in range(NW)] + [(2, w) for w in range(NW)]
+        with tc.manual_schedule(engines={mybir.EngineType.PE}):
+            waiting = []
+            direct = []
+            nxt_chunk = 0
+            for b in range(len(banks) // BLOCK):
+                mine = banks[BLOCK * b:BLOCK * (b + 1)]
+                tps = []
+                for g, w in mine:
+                    tps.append(turn(g, w))
+                for item in waiting:
+                    multiply(item)
+                waiting = []
+                for g, c in direct:
+                    waiting.append(quantize(g, c, grs[g][:, WIDE * c:WIDE * (c + 1)]))
+                direct = []
+                for i in range(P_AFTER[b]):
+                    g, n = chunks[nxt_chunk]
+                    nxt_chunk += 1
+                    interleave(g, n)
+                    if n == NLOAD - 1:
+                        for c in range(5):
+                            waiting.append(quantize(g, c, grs[g][:, WIDE * c:WIDE * (c + 1)]))
+                        direct = [(g, c) for c in range(5, NCHUNK)]
+                for (g, w), tp in zip(mine, tps):
+                    empty(g, w, tp)
+                    if w % 2 == 1:
+                        waiting.append(quantize(g, w // 2, gcs[g][:]))
+            for item in waiting:
+                multiply(item)
+            while nxt_chunk < len(chunks):
+                g, n = chunks[nxt_chunk]
+                nxt_chunk += 1
+                interleave(g, n)
+            for c in range(NCHUNK):
+                multiply(quantize(3, c, grs[3][:, WIDE * c:WIDE * (c + 1)]))
 
         m1 = const.tile([P, 1], F32)
         nc.vector.tensor_reduce(out=m1[:], in_=stat[:], axis=AX.X, op=ALU.max)

@@ -13,250 +13,263 @@ ACT = mybir.ActivationFunctionType
 ALU = mybir.AluOpType
 AX = mybir.AxisListType
 
-G, CO, CI, SF, L, KL = 4, 128, 512, 36, 256, 9
 P = 128
+PACK = 4
+GROUPS, CO, CI, L, TAPS, PAD = 4, 128, 512, 256, 9, 4
+SF = 36
 SEG_START = (0, 58, 116, 174)
 SEG_END = (58, 116, 174, 256)
 SEG_BASE = (0, 0, 64, 128)
-CHUNK = 4
-NCHUNK = SF // CHUNK
-NCO = 16
-NLOAD = CO // NCO
-AHEAD = 5
-V_CO = 14
-V_SHARE = {(3, 7): 10}
-BLOCK = 4
-P_AFTER = {0: 2, 1: 2, 2: 2, 3: 0, 4: 1, 5: 1, 6: 3, 7: 2, 8: 2}
-NW = SF // 2
-ROW_SLICES = 4
-V_BANKS = ()
 
-FLOPS = 2 * G * CO * CI * KL * L
+SF_PER_QUANT = 4
+QUANT_IN = SF_PER_QUANT * CO * PACK
+QUANTS = SF // SF_PER_QUANT
+WORDS = SF // 2
+
+DIRECT = (
+    [(1, 16 * i, 16, 0 if i == 0 else 16) for i in range(8)]
+    + [(3, 16 * i, 16, 14) for i in range(7)]
+    + [(3, 112, 8, 8), (3, 120, 8, 6)]
+)
+CHUNK_CO = 16
+GROUP1_LAST = 7
+AHEAD = 5
+LOADS = [0, "rows 0", 1, 2, 3, 4, 5, "rows 2"] + list(range(6, len(DIRECT)))
+
+BANKS = [(0, w) for w in range(WORDS)] + [(2, w) for w in range(WORDS)]
+BLOCK = 4
+CHUNKS_AFTER_BLOCK = (2, 2, 1, 0, 1, 1, 3, 2, 3)
+SPLIT = 5
+
+FLOPS = 2 * GROUPS * CO * CI * TAPS * L
 
 
 def tile_partiallyunsharedconv1d_pa_kernel(tc, x, weight, conv_bias_param, out_0, out_1):
     nc = tc.nc
-    w4 = weight.rearrange("d k o c s x f -> (d k) o (c s x f)")
-    xv = x.rearrange("o d k c l -> (o d k) c l").rearrange("g (p j) l -> p g (j l)", j=4)
-    bias_v = conv_bias_param.rearrange("d k o s x -> o (d k) (s x)")
-    out0_v = out_0.rearrange("o d k c l -> (o d k) c l")
-    out1_v = out_1.rearrange("o d k c l -> c (o d k) l")
+    w_rows = weight.rearrange("d k o c s x f -> (d k) o (c s x f)")
+    x_view = x.rearrange("o d k c l -> (o d k) c l").rearrange("g (p j) l -> p g (j l)", j=PACK)
+    bias_view = conv_bias_param.rearrange("d k o s x -> o (d k) (s x)")
+    out0_view = out_0.rearrange("o d k c l -> (o d k) c l")
+    out1_view = out_1.rearrange("o d k c l -> c (o d k) l")
 
     with ExitStack() as ctx:
         const = ctx.enter_context(tc.tile_pool(name="const", bufs=1))
-        rowp = ctx.enter_context(tc.tile_pool(name="rowp", bufs=2))
-        rawp = ctx.enter_context(tc.tile_pool(name="rawp", bufs=AHEAD + 1))
-        grp = ctx.enter_context(tc.tile_pool(name="grp", bufs=1))
-        gcp = ctx.enter_context(tc.tile_pool(name="gcp", bufs=4))
-        wqp = ctx.enter_context(tc.tile_pool(name="wqp", bufs=10))
-        pst = ctx.enter_context(tc.psum_pool(name="pst", bufs=6))
-        psa = ctx.enter_context(tc.psum_pool(name="psa", bufs=2))
+        row_pool = ctx.enter_context(tc.tile_pool(name="rows", bufs=2))
+        raw_pool = ctx.enter_context(tc.tile_pool(name="raw", bufs=AHEAD + 1))
+        big_pool = ctx.enter_context(tc.tile_pool(name="big", bufs=1))
+        part_pool = ctx.enter_context(tc.tile_pool(name="part", bufs=4))
+        code_pool = ctx.enter_context(tc.tile_pool(name="code", bufs=10))
+        turn_psum = ctx.enter_context(tc.psum_pool(name="turn", bufs=6))
+        acc_psum = ctx.enter_context(tc.psum_pool(name="acc", bufs=2))
 
-        stage = grp.tile([P, 2, G, 4 * L], BF16, tag="gr", align_bytes=64)
-        raw_x = stage[:, 0, :, :]
-        xg = stage[:, 1, :, :]
-        nc.sync.dma_start(out=raw_x, in_=xv)
-        bias_b = const.tile([P, G, 4], BF16)
-        nc.scalar.dma_start(out=bias_b[:], in_=bias_v)
+        stage = big_pool.tile([P, 2, GROUPS, PACK * L], BF16, tag="big", align_bytes=64)
+        x_raw = stage[:, 0, :, :]
+        x_grouped = stage[:, 1, :, :]
+        nc.sync.dma_start(out=x_raw, in_=x_view)
+        bias_bf = const.tile([P, GROUPS, 4], BF16)
+        nc.scalar.dma_start(out=bias_bf[:], in_=bias_view)
 
         rows = {}
         raws = {}
-
-        def load_rows(g):
-            row = rowp.tile([P, CI * SF], BF16, tag="row")
-            w = CI * SF // ROW_SLICES
-            for i in range(ROW_SLICES):
-                nc.sync.dma_start(out=row[:, w * i:w * (i + 1)], in_=w4[g, :, w * i:w * (i + 1)])
-            rows[g] = row
-
-        def load(g, n):
-            raw = rawp.tile([P, NCO, 4 * SF], BF16, tag="raw")
-            nc.sync.dma_start(out=raw[:], in_=w4[g, NCO * n:NCO * (n + 1), :].rearrange("c (p y) -> p c y", p=P))
-            raws[(g, n)] = raw
-
-        order = [(0, -1)] + [(1, n) for n in range(6)] + [(2, -1), (1, 6), (1, 7)] + [(3, n) for n in range(NLOAD)]
-        chunks = [item for item in order if item[1] >= 0]
         issued = []
 
-        def issue_until(item):
-            while item not in issued:
-                nxt = order[len(issued)]
-                if nxt[1] < 0:
-                    load_rows(nxt[0])
+        def issue_loads_until(index):
+            while index not in issued:
+                item = LOADS[len(issued)]
+                issued.append(item)
+                if item in ("rows 0", "rows 2"):
+                    g = 0 if item == "rows 0" else 2
+                    row = row_pool.tile([P, CI * SF], BF16, tag="row")
+                    quarter = CI * SF // 4
+                    for i in range(4):
+                        nc.sync.dma_start(out=row[:, quarter * i:quarter * (i + 1)],
+                                          in_=w_rows[g, :, quarter * i:quarter * (i + 1)])
+                    rows[g] = row
                 else:
-                    load(nxt[0], nxt[1])
-                issued.append(nxt)
+                    g, c0, n, n_vector = DIRECT[item]
+                    raw = raw_pool.tile([P, CHUNK_CO, PACK * SF], BF16, tag="raw")
+                    nc.sync.dma_start(out=raw[:, 0:n, :], in_=w_rows[g, c0:c0 + n, :].rearrange("c (p y) -> p c y", p=P))
+                    raws[item] = raw
 
-        issue_until(chunks[AHEAD - 1])
+        issue_loads_until(AHEAD - 1)
 
-        ident_f = const.tile([P, P], F32)
-        make_identity(nc, ident_f[:])
+        ident = const.tile([P, P], F32)
+        make_identity(nc, ident[:])
         zero = const.tile([P, 1], F32)
         nc.vector.memset(zero[:], 0.0)
-        bias_f = const.tile([P, G * 4], F32)
-        nc.vector.tensor_copy(out=bias_f[:], in_=bias_b[:].rearrange("p g s -> p (g s)"))
+        bias = const.tile([P, GROUPS * 4], F32)
+        nc.vector.tensor_copy(out=bias[:], in_=bias_bf[:].rearrange("p g s -> p (g s)"))
 
-        xc = const.tile([P, KL, G, L], I32, align_bytes=64)
-        xs = const.tile([P, KL, G, L], U8, align_bytes=64)
-        xc_fg = xc[:].rearrange("p f g j -> p (f g) j")
-        nc.vector.memset(xc_fg[:, :, 0:4], 0)
-        nc.vector.memset(xc_fg[:, :, L - 4:L], 0)
-        xs_w = xs[:].rearrange("p f g j -> p (f g) j").bitcast(I32)
-        nc.vector.memset(xs_w[:, :, 0:1], 0)
-        nc.vector.memset(xs_w[:, :, L // 4 - 1:L // 4], 0)
-        nc.vector.memset(xs[:, 4, :, :].bitcast(I32), 0)
-        for g in range(G):
-            dst = xg[:, g, :].rearrange("p (l j) -> p l j", j=4)
-            src = raw_x[:, g, :].rearrange("p (j l) -> p l j", j=4)
-            nc.scalar.copy(out=dst, in_=src)
-        for g in range(G):
-            nc.vector.quantize_mx(out=xc[:, 4, g, :].bitcast(FP8X4), scales=xs[:, 4, g, :], in_=xg[:, g, :])
-        for f in range(KL):
-            d = f - 4
-            if d == 0:
-                continue
-            lo, hi = max(0, -d), L - max(0, d)
-            nc.vector.tensor_copy(out=xc[:, f, :, lo:hi], in_=xc[:, 4, :, lo + d:hi + d])
+        x_codes = const.tile([P, TAPS, GROUPS, L], I32, align_bytes=64)
+        x_scales = const.tile([P, TAPS, GROUPS, L], U8, align_bytes=64)
+        codes_fg = x_codes[:].rearrange("p f g j -> p (f g) j")
+        scales_fg = x_scales[:].rearrange("p f g j -> p (f g) j").bitcast(I32)
+        scale_words = L // 4
+        nc.vector.memset(codes_fg[:, :, 0:PAD], 0)
+        nc.vector.memset(codes_fg[:, :, L - PAD:L], 0)
+        nc.vector.memset(scales_fg[:, :, 0:1], 0)
+        nc.vector.memset(scales_fg[:, :, scale_words - 1:scale_words], 0)
+        nc.vector.memset(x_scales[:, PAD, :, :].bitcast(I32), 0)
+        for g in range(GROUPS):
+            dst = x_grouped[:, g, :].rearrange("p (l j) -> p l j", j=PACK)
+            src = x_raw[:, g, :].rearrange("p (j l) -> p l j", j=PACK)
+            if g == 0:
+                nc.vector.tensor_copy(out=dst, in_=src)
+            else:
+                nc.scalar.copy(out=dst, in_=src)
+        for g in range(GROUPS):
+            nc.vector.quantize_mx(out=x_codes[:, PAD, g, :].bitcast(FP8X4), scales=x_scales[:, PAD, g, :],
+                                  in_=x_grouped[:, g, :])
+        for f in range(TAPS):
+            d = f - PAD
+            if d != 0:
+                lo, hi = max(0, -d), L - max(0, d)
+                nc.vector.tensor_copy(out=x_codes[:, f, :, lo:hi], in_=x_codes[:, PAD, :, lo + d:hi + d])
 
-        nw = L // 4
+        def scale_plane(f):
+            return x_scales[:, f, :, :].bitcast(I32)
+
         for d in (1, 2, 3):
-            nc.vector.tensor_copy(out=xs[:, 4 + d, :, 0:L - d], in_=xs[:, 4, :, d:L])
-        nc.vector.tensor_copy(out=xs[:, 8, :, :].bitcast(I32)[:, :, 0:nw - 1], in_=xs[:, 4, :, :].bitcast(I32)[:, :, 1:nw])
-        nc.vector.tensor_copy(out=xs[:, 0, :, :].bitcast(I32)[:, :, 1:nw], in_=xs[:, 4, :, :].bitcast(I32)[:, :, 0:nw - 1])
+            nc.vector.tensor_copy(out=x_scales[:, PAD + d, :, 0:L - d], in_=x_scales[:, PAD, :, d:L])
+        nc.vector.tensor_copy(out=scale_plane(2 * PAD)[:, :, 0:scale_words - 1], in_=scale_plane(PAD)[:, :, 1:scale_words])
+        nc.vector.tensor_copy(out=scale_plane(0)[:, :, 1:scale_words], in_=scale_plane(PAD)[:, :, 0:scale_words - 1])
         for d in (1, 2, 3):
-            nc.vector.tensor_copy(out=xs[:, d, :, :].bitcast(I32)[:, :, 1:nw], in_=xs[:, 4 + d, :, :].bitcast(I32)[:, :, 0:nw - 1])
-            nc.vector.tensor_copy(out=xs[:, d, :, 4 - d:4], in_=xs[:, 4, :, 0:d])
+            nc.vector.tensor_copy(out=scale_plane(d)[:, :, 1:scale_words], in_=scale_plane(PAD + d)[:, :, 0:scale_words - 1])
+            nc.vector.tensor_copy(out=x_scales[:, d, :, PAD - d:PAD], in_=x_scales[:, PAD, :, 0:d])
 
-        o_sb = const.tile([P, G, L], F32)
-        o8 = const.tile([P, G, L], FP8)
-        stat = const.tile([P, G], F32)
-        grs = {}
+        result = const.tile([P, GROUPS, L], F32)
+        result8 = const.tile([P, GROUPS, L], FP8)
+        peaks = const.tile([P, GROUPS + 1], F32)
+        grouped = {}
+        parts = {}
         accs = {}
 
-        def interleave(g, n):
-            if n == 0:
-                gr = grp.tile([P, SF * CO * 4], BF16, tag="gr", align_bytes=64)
-                grs[g] = gr
-            dst = grs[g][:].rearrange("p (s o j) -> p o s j", s=SF, j=4)
-            src = raws[(g, n)][:].rearrange("p c (j s) -> p c s j", j=4)
-            c0 = NCO * n
-            v = V_SHARE.get((g, n), V_CO)
-            if v > 0:
-                nc.vector.tensor_copy(out=dst[:, c0:c0 + v, :, :], in_=src[:, 0:v, :, :])
-            if v < NCO:
-                nc.scalar.copy(out=dst[:, c0 + v:c0 + NCO, :, :], in_=src[:, v:NCO, :, :])
-            pos = chunks.index((g, n)) + AHEAD
-            issue_until(chunks[min(pos, len(chunks) - 1)])
-
-        def finish_segment(g, s):
-            acc = accs[g]
-            a, st, en = SEG_BASE[s], SEG_START[s], SEG_END[s]
-            nc.scalar.activation(
-                out=o_sb[:, g, st:en], in_=acc[:, s, st - a:en - a], func=ACT.Identity,
-                bias=bias_f[:, 4 * g + s:4 * g + s + 1], scale=1.0,
-            )
-            if s == 3:
-                nc.scalar.dma_start(out=out0_v[g], in_=o_sb[:, g, :])
-                nc.vector.tensor_reduce(out=stat[:, g:g + 1], in_=o_sb[:, g, :], axis=AX.X, op=ALU.max,
-                                        apply_absolute_value=True)
-
-        def quantize(g, c, grouped):
-            wq = wqp.tile([P, CHUNK * CO], I32, tag="wq", align_bytes=64)
-            ws = wqp.tile([P, CHUNK * CO], U8, tag="ws", align_bytes=64)
-            nc.vector.quantize_mx(out=wq[:].bitcast(FP8X4), scales=ws[:], in_=grouped)
-            return (g, c, wq, ws)
-
-        def multiply(item):
-            g, c, wq, ws = item
-            if c == 0:
-                acc = psa.tile([P, 4, P], F32, tag="acc")
-                accs[g] = acc
-            acc = accs[g]
-            for i in range(CHUNK):
-                s, f = divmod(CHUNK * c + i, KL)
-                a = SEG_BASE[s]
-                nc.tensor.matmul_mx(
-                    out=acc[:, s, :],
-                    lhsT=wq[:, CO * i:CO * (i + 1)].bitcast(FP8X4), lhsT_scale=ws[:, CO * i:CO * (i + 1)],
-                    rhs=xc[:, f, g, a:a + P].bitcast(FP8X4), rhs_scale=xs[:, f, g, a:a + P],
-                    start=(f == 0), stop=(f == KL - 1),
-                )
-                if f == KL - 1:
-                    finish_segment(g, s)
-
-        WIDE = CHUNK * CO * 4
-        gcs = {}
+        def interleave(index):
+            g, c0, n, n_vector = DIRECT[index]
+            if c0 == 0:
+                big = big_pool.tile([P, SF * CO * PACK], BF16, tag="big", align_bytes=64)
+                grouped[g] = big
+            dst = grouped[g][:].rearrange("p (s o j) -> p o s j", s=SF, j=PACK)
+            src = raws[index][:].rearrange("p c (j s) -> p c s j", j=PACK)
+            if n_vector > 0:
+                nc.vector.tensor_copy(out=dst[:, c0:c0 + n_vector, :, :], in_=src[:, 0:n_vector, :, :])
+            if n_vector < n:
+                nc.scalar.copy(out=dst[:, c0 + n_vector:c0 + n, :, :], in_=src[:, n_vector:n, :, :])
+            issue_loads_until(min(index + AHEAD, len(DIRECT) - 1))
 
         def turn(g, w):
             words = rows[g][:].bitcast(F32)
-            tp = pst.tile([P, 4, P], F32, tag="tp")
-            for t in range(4):
-                first = t * NW + w
-                nc.tensor.transpose(tp[:, t, :], words[:, first:first + 4 * NW * 127 + 1:4 * NW], ident_f[:])
-            return tp
+            bank = turn_psum.tile([P, PACK, CO], F32, tag="bank")
+            step = PACK * WORDS
+            for t in range(PACK):
+                first = t * WORDS + w
+                nc.tensor.transpose(bank[:, t, :], words[:, first:first + step * (P - 1) + 1:step], ident[:])
+            return bank
 
-        def empty(g, w, tp):
+        def empty(g, w, bank):
             if w % 2 == 0:
-                gc = gcp.tile([P, WIDE], BF16, tag="gc", align_bytes=64)
-                gcs[g] = gc
-            gc = gcs[g]
-            half = WIDE // 2
-            dst = gc[:, half * (w % 2):half * (w % 2 + 1)].rearrange("p (e o t) -> p e o t", e=2, t=4)
-            src = tp[:].rearrange("p t o -> p (t o)").bitcast(BF16).rearrange("p (t o e) -> p e o t", t=4, e=2)
+                part = part_pool.tile([P, QUANT_IN], BF16, tag="part", align_bytes=64)
+                parts[g] = part
+            half = QUANT_IN // 2
+            dst = parts[g][:, half * (w % 2):half * (w % 2 + 1)].rearrange("p (e o t) -> p e o t", e=2, t=PACK)
+            src = bank[:].rearrange("p t o -> p (t o)").bitcast(BF16).rearrange("p (t o e) -> p e o t", t=PACK, e=2)
             nc.scalar.copy(out=dst, in_=src)
 
-        banks = [(0, w) for w in range(NW)] + [(2, w) for w in range(NW)]
+        def quantize(g, c, values):
+            codes = code_pool.tile([P, SF_PER_QUANT * CO], I32, tag="codes", align_bytes=64)
+            scales = code_pool.tile([P, SF_PER_QUANT * CO], U8, tag="scales", align_bytes=64)
+            nc.vector.quantize_mx(out=codes[:].bitcast(FP8X4), scales=scales[:], in_=values)
+            return (g, c, codes, scales)
+
+        def quantize_direct(g, c):
+            return quantize(g, c, grouped[g][:, QUANT_IN * c:QUANT_IN * (c + 1)])
+
+        def finish_segment(g, s):
+            base, start, end = SEG_BASE[s], SEG_START[s], SEG_END[s]
+            nc.scalar.activation(out=result[:, g, start:end], in_=accs[g][:, s, start - base:end - base], func=ACT.Identity,
+                                 bias=bias[:, 4 * g + s:4 * g + s + 1], scale=1.0)
+            if s == 3:
+                nc.scalar.dma_start(out=out0_view[g], in_=result[:, g, :])
+            if g < GROUPS - 1 and s == 3:
+                nc.vector.tensor_reduce(out=peaks[:, g:g + 1], in_=result[:, g, :], axis=AX.X, op=ALU.max,
+                                        apply_absolute_value=True)
+            if g == GROUPS - 1 and s == 2:
+                nc.vector.tensor_reduce(out=peaks[:, g:g + 1], in_=result[:, g, 0:end], axis=AX.X, op=ALU.max,
+                                        apply_absolute_value=True)
+            if g == GROUPS - 1 and s == 3:
+                nc.vector.tensor_reduce(out=peaks[:, g + 1:g + 2], in_=result[:, g, start:end], axis=AX.X, op=ALU.max,
+                                        apply_absolute_value=True)
+
+        def multiply(item):
+            g, c, codes, scales = item
+            if c == 0:
+                acc = acc_psum.tile([P, 4, P], F32, tag="acc")
+                accs[g] = acc
+            for i in range(SF_PER_QUANT):
+                s, f = divmod(SF_PER_QUANT * c + i, TAPS)
+                base = SEG_BASE[s]
+                nc.tensor.matmul_mx(
+                    out=accs[g][:, s, :],
+                    lhsT=codes[:, CO * i:CO * (i + 1)].bitcast(FP8X4), lhsT_scale=scales[:, CO * i:CO * (i + 1)],
+                    rhs=x_codes[:, f, g, base:base + P].bitcast(FP8X4), rhs_scale=x_scales[:, f, g, base:base + P],
+                    start=(f == 0), stop=(f == TAPS - 1),
+                )
+                if f == TAPS - 1:
+                    finish_segment(g, s)
+
         with tc.manual_schedule(engines={mybir.EngineType.PE}):
+            interleave(0)
+            chunk = 1
             waiting = []
-            direct = []
-            nxt_chunk = 0
-            for b in range(len(banks) // BLOCK):
-                mine = banks[BLOCK * b:BLOCK * (b + 1)]
-                tps = []
+            postponed = []
+            n_blocks = len(BANKS) // BLOCK
+            for b in range(n_blocks):
+                mine = BANKS[BLOCK * b:BLOCK * (b + 1)]
+                banks = []
                 for g, w in mine:
-                    tps.append(turn(g, w))
+                    banks.append(turn(g, w))
                 for item in waiting:
                     multiply(item)
                 waiting = []
-                for g, c in direct:
-                    waiting.append(quantize(g, c, grs[g][:, WIDE * c:WIDE * (c + 1)]))
-                direct = []
-                for i in range(P_AFTER[b]):
-                    g, n = chunks[nxt_chunk]
-                    nxt_chunk += 1
-                    interleave(g, n)
-                    if n == NLOAD - 1:
-                        for c in range(5):
-                            waiting.append(quantize(g, c, grs[g][:, WIDE * c:WIDE * (c + 1)]))
-                        direct = [(g, c) for c in range(5, NCHUNK)]
-                for (g, w), tp in zip(mine, tps):
-                    empty(g, w, tp)
-                    if w % 2 == 1:
-                        waiting.append(quantize(g, w // 2, gcs[g][:]))
-            for item in waiting:
-                multiply(item)
-            while nxt_chunk < len(chunks):
-                g, n = chunks[nxt_chunk]
-                nxt_chunk += 1
-                interleave(g, n)
-            for c in range(NCHUNK):
-                multiply(quantize(3, c, grs[3][:, WIDE * c:WIDE * (c + 1)]))
+                for g, c in postponed:
+                    waiting.append(quantize_direct(g, c))
+                postponed = []
+                for i in range(CHUNKS_AFTER_BLOCK[b]):
+                    interleave(chunk)
+                    if chunk == GROUP1_LAST:
+                        for c in range(SPLIT):
+                            waiting.append(quantize_direct(1, c))
+                        postponed = [(1, c) for c in range(SPLIT, QUANTS)]
+                    chunk += 1
+                late = []
+                for (g, w), bank in zip(mine, banks):
+                    empty(g, w, bank)
+                    if w % 2 == 1 and b < n_blocks - 1:
+                        waiting.append(quantize(g, w // 2, parts[g][:]))
+                    elif w % 2 == 1:
+                        late.append((g, w // 2, parts[g]))
+            interleave(chunk)
+            for c in range(QUANTS):
+                if c == SPLIT - 1:
+                    for g, cc, part in late:
+                        multiply(quantize(g, cc, part[:]))
+                multiply(quantize_direct(3, c))
 
-        m1 = const.tile([P, 1], F32)
-        nc.vector.tensor_reduce(out=m1[:], in_=stat[:], axis=AX.X, op=ALU.max)
-        spread = pst.tile([P, P], F32, tag="tp")
-        nc.tensor.transpose(spread[:], m1[:, 0:1].to_broadcast([P, P]), ident_f[:])
-        amax = const.tile([P, 1], F32)
-        nc.vector.tensor_reduce(out=amax[:], in_=spread[:], axis=AX.X, op=ALU.max)
-        rec = const.tile([P, 1], F32)
-        nc.vector.reciprocal(out=rec[:], in_=amax[:])
-        fac = const.tile([P, 1], F32)
-        nc.vector.tensor_scalar(out=fac[:], in0=rec[:], scalar1=448.0, scalar2=None, op0=ALU.mult)
-        nc.scalar.activation(out=o8[:, 3, :], in_=o_sb[:, 3, :], func=ACT.Identity, scale=fac[:, 0:1],
+        scaled = const.tile([P, GROUPS + 1], F32)
+        mine_max = const.tile([P, 1], F32)
+        nc.vector.tensor_scalar(out=scaled[:], in0=peaks[:], scalar1=1.0 / 448.0, scalar2=None, op0=ALU.mult, op1=ALU.max,
+                                accum_out=mine_max[:])
+        spread = turn_psum.tile([P, P], F32, tag="bank")
+        nc.tensor.transpose(spread[:], mine_max[:, 0:1].to_broadcast([P, P]), ident[:])
+        scale = const.tile([P, 1], F32)
+        nc.vector.tensor_reduce(out=scale[:], in_=spread[:], axis=AX.X, op=ALU.max)
+        factor = const.tile([P, 1], F32)
+        nc.vector.reciprocal(out=factor[:], in_=scale[:])
+        nc.scalar.activation(out=result8[:, 3, :], in_=result[:, 3, :], func=ACT.Identity, scale=factor[:, 0:1],
                              bias=zero[:, 0:1], saturate=False)
-        nc.vector.tensor_scalar(out=o8[:, 0:2, :], in0=o_sb[:, 0:2, :], scalar1=fac[:, 0:1], scalar2=None,
+        nc.vector.tensor_scalar(out=result8[:, 0:2, :], in0=result[:, 0:2, :], scalar1=factor[:, 0:1], scalar2=None,
                                 op0=ALU.mult, saturate=False)
-        nc.sync.dma_start(out=out1_v[:, 0:2, :], in_=o8[:, 0:2, :].bitcast(U8))
-        nc.vector.tensor_scalar(out=o8[:, 2, :], in0=o_sb[:, 2, :], scalar1=fac[:, 0:1], scalar2=None,
+        nc.sync.dma_start(out=out1_view[:, 0:2, :], in_=result8[:, 0:2, :].bitcast(U8))
+        nc.vector.tensor_scalar(out=result8[:, 2, :], in0=result[:, 2, :], scalar1=factor[:, 0:1], scalar2=None,
                                 op0=ALU.mult, saturate=False)
-        nc.sync.dma_start(out=out1_v[:, 2:4, :], in_=o8[:, 2:4, :].bitcast(U8))
+        nc.sync.dma_start(out=out1_view[:, 2:4, :], in_=result8[:, 2:4, :].bitcast(U8))

@@ -21,9 +21,9 @@ SEG_START = (0, 58, 116, 174)
 SEG_END = (58, 116, 174, 256)
 SEG_BASE = (0, 0, 64, 128)
 
-SF_PER_QUANT = 4
-QUANT_IN = SF_PER_QUANT * CO * PACK
-QUANTS = SF // SF_PER_QUANT
+SF_IN = CO * PACK
+WIDE_CALLS = ((0, 8), (8, 8), (16, 8), (24, 8), (32, 4))
+NARROW_CALLS = tuple([(4 * c, 4) for c in range(9)])
 WORDS = SF // 2
 
 DIRECT = (
@@ -39,7 +39,7 @@ LOADS = [0, "rows 0", 1, 2, 3, 4, 5, "rows 2"] + list(range(6, len(DIRECT)))
 BANKS = [(0, w) for w in range(WORDS)] + [(2, w) for w in range(WORDS)]
 BLOCK = 4
 CHUNKS_AFTER_BLOCK = (2, 2, 1, 0, 1, 1, 3, 2, 3)
-SPLIT = 5
+SPLIT = 3
 
 FLOPS = 2 * GROUPS * CO * CI * TAPS * L
 
@@ -57,8 +57,8 @@ def tile_partiallyunsharedconv1d_pa_kernel(tc, x, weight, conv_bias_param, out_0
         row_pool = ctx.enter_context(tc.tile_pool(name="rows", bufs=2))
         raw_pool = ctx.enter_context(tc.tile_pool(name="raw", bufs=AHEAD + 1))
         big_pool = ctx.enter_context(tc.tile_pool(name="big", bufs=1))
-        part_pool = ctx.enter_context(tc.tile_pool(name="part", bufs=4))
-        code_pool = ctx.enter_context(tc.tile_pool(name="code", bufs=10))
+        part_pool = ctx.enter_context(tc.tile_pool(name="part", bufs=2))
+        code_pool = ctx.enter_context(tc.tile_pool(name="code", bufs=6))
         turn_psum = ctx.enter_context(tc.psum_pool(name="turn", bufs=6))
         acc_psum = ctx.enter_context(tc.psum_pool(name="acc", bufs=2))
 
@@ -141,7 +141,6 @@ def tile_partiallyunsharedconv1d_pa_kernel(tc, x, weight, conv_bias_param, out_0
         result8 = const.tile([P, GROUPS, L], FP8)
         peaks = const.tile([P, GROUPS + 1], F32)
         grouped = {}
-        parts = {}
         accs = {}
 
         def interleave(index):
@@ -166,23 +165,20 @@ def tile_partiallyunsharedconv1d_pa_kernel(tc, x, weight, conv_bias_param, out_0
                 nc.tensor.transpose(bank[:, t, :], words[:, first:first + step * (P - 1) + 1:step], ident[:])
             return bank
 
-        def empty(g, w, bank):
-            if w % 2 == 0:
-                part = part_pool.tile([P, QUANT_IN], BF16, tag="part", align_bytes=64)
-                parts[g] = part
-            half = QUANT_IN // 2
-            dst = parts[g][:, half * (w % 2):half * (w % 2 + 1)].rearrange("p (e o t) -> p e o t", e=2, t=PACK)
+        def empty(bank, part, i):
+            dst = part[:, 2 * SF_IN * i:2 * SF_IN * (i + 1)].rearrange("p (e o t) -> p e o t", e=2, t=PACK)
             src = bank[:].rearrange("p t o -> p (t o)").bitcast(BF16).rearrange("p (t o e) -> p e o t", t=PACK, e=2)
             nc.scalar.copy(out=dst, in_=src)
 
-        def quantize(g, c, values):
-            codes = code_pool.tile([P, SF_PER_QUANT * CO], I32, tag="codes", align_bytes=64)
-            scales = code_pool.tile([P, SF_PER_QUANT * CO], U8, tag="scales", align_bytes=64)
-            nc.vector.quantize_mx(out=codes[:].bitcast(FP8X4), scales=scales[:], in_=values)
-            return (g, c, codes, scales)
+        def quantize(g, sf0, n, values):
+            codes = code_pool.tile([P, 8 * CO], I32, tag="codes", align_bytes=64)
+            scales = code_pool.tile([P, 8 * CO], U8, tag="scales", align_bytes=64)
+            nc.vector.quantize_mx(out=codes[:, 0:n * CO].bitcast(FP8X4), scales=scales[:, 0:n * CO], in_=values)
+            return (g, sf0, n, codes, scales)
 
-        def quantize_direct(g, c):
-            return quantize(g, c, grouped[g][:, QUANT_IN * c:QUANT_IN * (c + 1)])
+        def quantize_direct(g, call):
+            sf0, n = call
+            return quantize(g, sf0, n, grouped[g][:, SF_IN * sf0:SF_IN * (sf0 + n)])
 
         def finish_segment(g, s):
             base, start, end = SEG_BASE[s], SEG_START[s], SEG_END[s]
@@ -201,12 +197,12 @@ def tile_partiallyunsharedconv1d_pa_kernel(tc, x, weight, conv_bias_param, out_0
                                         apply_absolute_value=True)
 
         def multiply(item):
-            g, c, codes, scales = item
-            if c == 0:
+            g, sf0, n, codes, scales = item
+            if sf0 == 0:
                 acc = acc_psum.tile([P, 4, P], F32, tag="acc")
                 accs[g] = acc
-            for i in range(SF_PER_QUANT):
-                s, f = divmod(SF_PER_QUANT * c + i, TAPS)
+            for i in range(n):
+                s, f = divmod(sf0 + i, TAPS)
                 base = SEG_BASE[s]
                 nc.tensor.matmul_mx(
                     out=accs[g][:, s, :],
@@ -221,7 +217,7 @@ def tile_partiallyunsharedconv1d_pa_kernel(tc, x, weight, conv_bias_param, out_0
             interleave(0)
             chunk = 1
             waiting = []
-            postponed = []
+            postponed = ()
             n_blocks = len(BANKS) // BLOCK
             for b in range(n_blocks):
                 mine = BANKS[BLOCK * b:BLOCK * (b + 1)]
@@ -231,29 +227,34 @@ def tile_partiallyunsharedconv1d_pa_kernel(tc, x, weight, conv_bias_param, out_0
                 for item in waiting:
                     multiply(item)
                 waiting = []
-                for g, c in postponed:
-                    waiting.append(quantize_direct(g, c))
-                postponed = []
+                for call in postponed:
+                    waiting.append(quantize_direct(1, call))
+                postponed = ()
                 for i in range(CHUNKS_AFTER_BLOCK[b]):
                     interleave(chunk)
                     if chunk == GROUP1_LAST:
-                        for c in range(SPLIT):
-                            waiting.append(quantize_direct(1, c))
-                        postponed = [(1, c) for c in range(SPLIT, QUANTS)]
+                        for call in WIDE_CALLS[:SPLIT]:
+                            waiting.append(quantize_direct(1, call))
+                        postponed = WIDE_CALLS[SPLIT:]
                     chunk += 1
                 late = []
-                for (g, w), bank in zip(mine, banks):
-                    empty(g, w, bank)
-                    if w % 2 == 1 and b < n_blocks - 1:
-                        waiting.append(quantize(g, w // 2, parts[g][:]))
-                    elif w % 2 == 1:
-                        late.append((g, w // 2, parts[g]))
+                for g in (0, 2):
+                    some = [(w, bank) for (gg, w), bank in zip(mine, banks) if gg == g]
+                    if len(some) > 0:
+                        part = part_pool.tile([P, 8 * SF_IN], BF16, tag="part", align_bytes=64)
+                        for i, (w, bank) in enumerate(some):
+                            empty(bank, part, i)
+                        unit = (g, 2 * some[0][0], 2 * len(some), part[:, 0:2 * len(some) * SF_IN])
+                        if b < n_blocks - 1:
+                            waiting.append(quantize(unit[0], unit[1], unit[2], unit[3]))
+                        else:
+                            late.append(unit)
             interleave(chunk)
-            for c in range(QUANTS):
-                if c == SPLIT - 1:
-                    for g, cc, part in late:
-                        multiply(quantize(g, cc, part[:]))
-                multiply(quantize_direct(3, c))
+            for i, call in enumerate(NARROW_CALLS):
+                if i == 4:
+                    for unit in late:
+                        multiply(quantize(unit[0], unit[1], unit[2], unit[3]))
+                multiply(quantize_direct(3, call))
 
         scaled = const.tile([P, GROUPS + 1], F32)
         mine_max = const.tile([P, 1], F32)

@@ -27,14 +27,14 @@ NARROW_CALLS = tuple([(4 * c, 4) for c in range(9)])
 WORDS = SF // 2
 
 DIRECT = (
-    [(1, 16 * i, 16, 0 if i == 0 else 16) for i in range(8)]
+    [(1, 16 * i, 16, 16) for i in range(8)]
     + [(3, 16 * i, 16, 14) for i in range(7)]
     + [(3, 112, 8, 8), (3, 120, 8, 6)]
 )
 CHUNK_CO = 16
 GROUP1_LAST = 7
 AHEAD = 5
-LOADS = [0, "rows 0", 1, 2, 3, 4, 5, "rows 2"] + list(range(6, len(DIRECT)))
+LOADS = ["rows 0", 0, 1, 2, 3, 4, "rows 2"] + list(range(5, len(DIRECT)))
 
 BANKS = [(0, w) for w in range(WORDS)] + [(2, w) for w in range(WORDS)]
 BLOCK = 4

@@ -23,22 +23,23 @@ SEG_BASE = (0, 0, 64, 128)
 
 SF_IN = CO * PACK
 WIDE_CALLS = ((0, 8), (8, 8), (16, 8), (24, 8), (32, 4))
-NARROW_CALLS = tuple([(4 * c, 4) for c in range(9)])
+NARROW_CALLS = tuple([(4 * c, 4) for c in range(8)]) + ((32, 2), (34, 2))
 WORDS = SF // 2
 
 DIRECT = (
-    [(1, 16 * i, 16, 16) for i in range(8)]
-    + [(3, 16 * i, 16, 14) for i in range(7)]
-    + [(3, 112, 8, 8), (3, 120, 8, 6)]
+    [(1, 16 * i, 16, 16) for i in range(7)]
+    + [(1, 112, 12, 12), (1, 124, 4, 4)]
+    + [(3, 16 * i, 16, 12 if i < 4 else 16) for i in range(7)]
+    + [(3, 112, 12, 12), (3, 124, 4, 4)]
 )
 CHUNK_CO = 16
-GROUP1_LAST = 7
+GROUP1_LAST = 8
 AHEAD = 5
 LOADS = ["rows 0", 0, 1, 2, 3, 4, "rows 2"] + list(range(5, len(DIRECT)))
 
 BANKS = [(0, w) for w in range(WORDS)] + [(2, w) for w in range(WORDS)]
 BLOCK = 4
-CHUNKS_AFTER_BLOCK = (2, 2, 1, 0, 1, 1, 3, 2, 3)
+CHUNKS_AFTER_BLOCK = (2, 2, 1, 0, 1, 2, 3, 2, 3)
 SPLIT = 3
 
 FLOPS = 2 * GROUPS * CO * CI * TAPS * L
@@ -137,9 +138,10 @@ def tile_partiallyunsharedconv1d_pa_kernel(tc, x, weight, conv_bias_param, out_0
             nc.vector.tensor_copy(out=scale_plane(d)[:, :, 1:scale_words], in_=scale_plane(PAD + d)[:, :, 0:scale_words - 1])
             nc.vector.tensor_copy(out=x_scales[:, d, :, PAD - d:PAD], in_=x_scales[:, PAD, :, 0:d])
 
-        result = const.tile([P, GROUPS, L], F32)
+        result_all = const.tile([P, GROUPS * L + 1], F32)
+        result = result_all[:, 0:GROUPS * L].rearrange("p (g l) -> p g l", g=GROUPS)
         result8 = const.tile([P, GROUPS, L], FP8)
-        peaks = const.tile([P, GROUPS + 1], F32)
+        peaks = const.tile([P, GROUPS], F32)
         grouped = {}
         accs = {}
 
@@ -186,15 +188,12 @@ def tile_partiallyunsharedconv1d_pa_kernel(tc, x, weight, conv_bias_param, out_0
                                  bias=bias[:, 4 * g + s:4 * g + s + 1], scale=1.0)
             if s == 3:
                 nc.scalar.dma_start(out=out0_view[g], in_=result[:, g, :])
-            if g < GROUPS - 1 and s == 3:
-                nc.vector.tensor_reduce(out=peaks[:, g:g + 1], in_=result[:, g, :], axis=AX.X, op=ALU.max,
-                                        apply_absolute_value=True)
-            if g == GROUPS - 1 and s == 2:
-                nc.vector.tensor_reduce(out=peaks[:, g:g + 1], in_=result[:, g, 0:end], axis=AX.X, op=ALU.max,
-                                        apply_absolute_value=True)
-            if g == GROUPS - 1 and s == 3:
-                nc.vector.tensor_reduce(out=peaks[:, g + 1:g + 2], in_=result[:, g, start:end], axis=AX.X, op=ALU.max,
-                                        apply_absolute_value=True)
+            if g < 2 and s == 3:
+                peak(g, L)
+
+        def peak(g, end):
+            nc.vector.tensor_reduce(out=peaks[:, g:g + 1], in_=result[:, g, 0:end], axis=AX.X, op=ALU.max,
+                                    apply_absolute_value=True)
 
         def multiply(item):
             g, sf0, n, codes, scales = item
@@ -256,14 +255,20 @@ def tile_partiallyunsharedconv1d_pa_kernel(tc, x, weight, conv_bias_param, out_0
                         multiply(quantize(unit[0], unit[1], unit[2], unit[3]))
                 multiply(quantize_direct(3, call))
 
-        scaled = const.tile([P, GROUPS + 1], F32)
+        peak(2, L)
+        peak(3, SEG_START[3])
+        copied = const.tile([P, GROUPS], F32)
+        nc.vector.tensor_scalar(out=copied[:], in0=peaks[:], scalar1=1.0, scalar2=None, op0=ALU.mult, op1=ALU.max,
+                                accum_out=result_all[:, GROUPS * L:GROUPS * L + 1])
         mine_max = const.tile([P, 1], F32)
-        nc.vector.tensor_scalar(out=scaled[:], in0=peaks[:], scalar1=1.0 / 448.0, scalar2=None, op0=ALU.mult, op1=ALU.max,
-                                accum_out=mine_max[:])
+        nc.vector.tensor_reduce(out=mine_max[:], in_=result_all[:, 3 * L + SEG_START[3]:GROUPS * L + 1], axis=AX.X, op=ALU.max,
+                                apply_absolute_value=True)
         spread = turn_psum.tile([P, P], F32, tag="bank")
         nc.tensor.transpose(spread[:], mine_max[:, 0:1].to_broadcast([P, P]), ident[:])
         scale = const.tile([P, 1], F32)
-        nc.vector.tensor_reduce(out=scale[:], in_=spread[:], axis=AX.X, op=ALU.max)
+        scaled = const.tile([P, P], F32)
+        nc.vector.tensor_scalar(out=scaled[:], in0=spread[:], scalar1=1.0 / 448.0, scalar2=None, op0=ALU.mult, op1=ALU.max,
+                                accum_out=scale[:])
         factor = const.tile([P, 1], F32)
         nc.vector.reciprocal(out=factor[:], in_=scale[:])
         nc.scalar.activation(out=result8[:, 3, :], in_=result[:, 3, :], func=ACT.Identity, scale=factor[:, 0:1],

@@ -34,6 +34,7 @@ DIRECT = (
 )
 CHUNK_CO = 16
 GROUP1_LAST = 8
+RUN = 4
 AHEAD = 5
 LOADS = ["rows 0", 0, 1, 2, 3, 4, "rows 2"] + list(range(5, len(DIRECT)))
 
@@ -150,12 +151,13 @@ def tile_partiallyunsharedconv1d_pa_kernel(tc, x, weight, conv_bias_param, out_0
             if c0 == 0:
                 big = big_pool.tile([P, SF * CO * PACK], BF16, tag="big", align_bytes=64)
                 grouped[g] = big
-            dst = grouped[g][:].rearrange("p (s o j) -> p o s j", s=SF, j=PACK)
-            src = raws[index][:].rearrange("p c (j s) -> p c s j", j=PACK)
+            dst = grouped[g][:].rearrange("p (a b y) -> p a y b", a=SF // RUN, b=RUN)
+            src = raws[index][:].rearrange("p c y -> p (c y)").rearrange("p (x a b) -> p a x b", a=SF // RUN, b=RUN)
             if n_vector > 0:
-                nc.vector.tensor_copy(out=dst[:, c0:c0 + n_vector, :, :], in_=src[:, 0:n_vector, :, :])
+                nc.vector.tensor_copy(out=dst[:, :, PACK * c0:PACK * (c0 + n_vector), :], in_=src[:, :, 0:PACK * n_vector, :])
             if n_vector < n:
-                nc.scalar.copy(out=dst[:, c0 + n_vector:c0 + n, :, :], in_=src[:, n_vector:n, :, :])
+                nc.scalar.copy(out=dst[:, :, PACK * (c0 + n_vector):PACK * (c0 + n), :],
+                               in_=src[:, :, PACK * n_vector:PACK * n, :])
             issue_loads_until(min(index + AHEAD, len(DIRECT) - 1))
 
         def turn(g, w):

@@ -36,7 +36,7 @@ CHUNK_CO = 16
 GROUP1_LAST = 8
 RUN = 4
 AHEAD = 5
-LOADS = ["rows 0", 0, 1, 2, 3, 4, "rows 2"] + list(range(5, len(DIRECT)))
+LOADS = ["rows 0", 0, 1, 2, "rows 2"] + list(range(3, len(DIRECT)))
 
 BANKS = [(0, w) for w in range(WORDS)] + [(2, w) for w in range(WORDS)]
 BLOCK = 4
@@ -199,6 +199,7 @@ def tile_partiallyunsharedconv1d_pa_kernel(tc, x, weight, conv_bias_param, out_0
 
         def multiply(item):
             g, sf0, n, codes, scales = item
+            closed = []
             if sf0 == 0:
                 acc = acc_psum.tile([P, 4, P], F32, tag="acc")
                 accs[g] = acc
@@ -212,7 +213,17 @@ def tile_partiallyunsharedconv1d_pa_kernel(tc, x, weight, conv_bias_param, out_0
                     start=(f == 0), stop=(f == TAPS - 1),
                 )
                 if f == TAPS - 1:
-                    finish_segment(g, s)
+                    closed.append((g, s))
+            return closed
+
+        def multiply_all(items):
+            closed = []
+            for i, item in enumerate(items):
+                closed.extend(multiply(item))
+                if i + 1 == len(items) or items[i + 1][0] != item[0]:
+                    for g, s in closed:
+                        finish_segment(g, s)
+                    closed = []
 
         with tc.manual_schedule(engines={mybir.EngineType.PE}):
             interleave(0)
@@ -225,8 +236,7 @@ def tile_partiallyunsharedconv1d_pa_kernel(tc, x, weight, conv_bias_param, out_0
                 banks = []
                 for g, w in mine:
                     banks.append(turn(g, w))
-                for item in waiting:
-                    multiply(item)
+                multiply_all(waiting)
                 waiting = []
                 for call in postponed:
                     waiting.append(quantize_direct(1, call))
@@ -254,8 +264,8 @@ def tile_partiallyunsharedconv1d_pa_kernel(tc, x, weight, conv_bias_param, out_0
             for i, call in enumerate(NARROW_CALLS):
                 if i == 4:
                     for unit in late:
-                        multiply(quantize(unit[0], unit[1], unit[2], unit[3]))
-                multiply(quantize_direct(3, call))
+                        multiply_all([quantize(unit[0], unit[1], unit[2], unit[3])])
+                multiply_all([quantize_direct(3, call)])
 
         peak(2, L)
         peak(3, SEG_START[3])

@@ -154,7 +154,9 @@ def tile_partiallyunsharedconv1d_pa_kernel(tc, x, weight, conv_bias_param, out_0
             dst = grouped[g][:].rearrange("p (a b y) -> p a y b", a=SF // RUN, b=RUN)
             src = raws[index][:].rearrange("p c y -> p (c y)").rearrange("p (x a b) -> p a x b", a=SF // RUN, b=RUN)
             if n_vector > 0:
-                nc.vector.tensor_copy(out=dst[:, :, PACK * c0:PACK * (c0 + n_vector), :], in_=src[:, :, 0:PACK * n_vector, :])
+                nc.vector.tensor_copy(
+                    out=dst[:, :, PACK * c0:PACK * (c0 + n_vector), :].rearrange("p a (h y) b -> p h a y b", h=2),
+                    in_=src[:, :, 0:PACK * n_vector, :].rearrange("p a (h y) b -> p h a y b", h=2))
             if n_vector < n:
                 nc.scalar.copy(out=dst[:, :, PACK * (c0 + n_vector):PACK * (c0 + n), :],
                                in_=src[:, :, PACK * n_vector:PACK * n, :])

@@ -264,7 +264,7 @@ def tile_partiallyunsharedconv1d_pa_kernel(tc, x, weight, conv_bias_param, out_0
                             late.append(unit)
             interleave(chunk)
             for i, call in enumerate(NARROW_CALLS):
-                if i == 4:
+                if i == 7:
                     for unit in late:
                         multiply_all([quantize(unit[0], unit[1], unit[2], unit[3])])
                 multiply_all([quantize_direct(3, call)])

from contextlib import ExitStack

import concourse.mybir as mybir
from concourse.masks import make_identity

F32 = mybir.dt.float32
BF16 = mybir.dt.bfloat16
I32 = mybir.dt.int32
U8 = mybir.dt.uint8
FP8 = mybir.dt.float8_e4m3fn
FP8X4 = mybir.dt.float8_e4m3fn_x4
ACT = mybir.ActivationFunctionType
ALU = mybir.AluOpType
AX = mybir.AxisListType

P = 128
PACK = 4
GROUPS, CO, CI, L, TAPS, PAD = 4, 128, 512, 256, 9, 4
SF = 36
SEG_START = (0, 58, 116, 174)
SEG_END = (58, 116, 174, 256)
SEG_BASE = (0, 0, 64, 128)

SF_IN = CO * PACK
WIDE_CALLS = ((0, 8), (8, 8), (16, 8), (24, 8), (32, 4))
NARROW_CALLS = tuple([(4 * c, 4) for c in range(8)]) + ((32, 2), (34, 2))
WORDS = SF // 2

DIRECT = (
    [(1, 16 * i, 16, 16) for i in range(7)]
    + [(1, 112, 12, 12), (1, 124, 4, 4)]
    + [(3, 16 * i, 16, 12 if i < 4 else 16) for i in range(7)]
    + [(3, 112, 12, 12), (3, 124, 4, 4)]
)
CHUNK_CO = 16
GROUP1_LAST = 8
RUN = 4
AHEAD = 5
LOADS = ["rows 0", 0, 1, 2, "rows 2"] + list(range(3, len(DIRECT)))

BANKS = [(0, w) for w in range(WORDS)] + [(2, w) for w in range(WORDS)]
BLOCK = 4
CHUNKS_AFTER_BLOCK = (2, 2, 1, 0, 1, 2, 3, 2, 3)
SPLIT = 3

FLOPS = 2 * GROUPS * CO * CI * TAPS * L


def tile_partiallyunsharedconv1d_pa_kernel(tc, x, weight, conv_bias_param, out_0, out_1):
    nc = tc.nc
    w_rows = weight.rearrange("d k o c s x f -> (d k) o (c s x f)")
    x_view = x.rearrange("o d k c l -> (o d k) c l").rearrange("g (p j) l -> p g (j l)", j=PACK)
    bias_view = conv_bias_param.rearrange("d k o s x -> o (d k) (s x)")
    out0_view = out_0.rearrange("o d k c l -> (o d k) c l")
    out1_view = out_1.rearrange("o d k c l -> c (o d k) l")

    with ExitStack() as ctx:
        const = ctx.enter_context(tc.tile_pool(name="const", bufs=1))
        row_pool = ctx.enter_context(tc.tile_pool(name="rows", bufs=2))
        raw_pool = ctx.enter_context(tc.tile_pool(name="raw", bufs=AHEAD + 1))
        big_pool = ctx.enter_context(tc.tile_pool(name="big", bufs=1))
        part_pool = ctx.enter_context(tc.tile_pool(name="part", bufs=2))
        code_pool = ctx.enter_context(tc.tile_pool(name="code", bufs=6))
        turn_psum = ctx.enter_context(tc.psum_pool(name="turn", bufs=6))
        acc_psum = ctx.enter_context(tc.psum_pool(name="acc", bufs=2))

        stage = big_pool.tile([P, 2, GROUPS, PACK * L], BF16, tag="big", align_bytes=64)
        x_raw = stage[:, 0, :, :]
        x_grouped = stage[:, 1, :, :]
        nc.sync.dma_start(out=x_raw, in_=x_view)
        bias_bf = const.tile([P, GROUPS, 4], BF16)
        nc.scalar.dma_start(out=bias_bf[:], in_=bias_view)

        rows = {}
        raws = {}
        issued = []

        def issue_loads_until(index):
            while index not in issued:
                item = LOADS[len(issued)]
                issued.append(item)
                if item in ("rows 0", "rows 2"):
                    g = 0 if item == "rows 0" else 2
                    row = row_pool.tile([P, CI * SF], BF16, tag="row")
                    quarter = CI * SF // 4
                    for i in range(4):
                        nc.sync.dma_start(out=row[:, quarter * i:quarter * (i + 1)],
                                          in_=w_rows[g, :, quarter * i:quarter * (i + 1)])
                    rows[g] = row
                else:
                    g, c0, n, n_vector = DIRECT[item]
                    raw = raw_pool.tile([P, CHUNK_CO, PACK * SF], BF16, tag="raw")
                    nc.sync.dma_start(out=raw[:, 0:n, :], in_=w_rows[g, c0:c0 + n, :].rearrange("c (p y) -> p c y", p=P))
                    raws[item] = raw

        issue_loads_until(AHEAD - 1)

        ident = const.tile([P, P], F32)
        make_identity(nc, ident[:])
        zero = const.tile([P, 1], F32)
        nc.vector.memset(zero[:], 0.0)
        bias = const.tile([P, GROUPS * 4], F32)
        nc.vector.tensor_copy(out=bias[:], in_=bias_bf[:].rearrange("p g s -> p (g s)"))

        x_codes = const.tile([P, TAPS, GROUPS, L], I32, align_bytes=64)
        x_scales = const.tile([P, TAPS, GROUPS, L], U8, align_bytes=64)
        codes_fg = x_codes[:].rearrange("p f g j -> p (f g) j")
        scales_fg = x_scales[:].rearrange("p f g j -> p (f g) j").bitcast(I32)
        scale_words = L // 4
        nc.vector.memset(codes_fg[:, :, 0:PAD], 0)
        nc.vector.memset(codes_fg[:, :, L - PAD:L], 0)
        nc.vector.memset(scales_fg[:, :, 0:1], 0)
        nc.vector.memset(scales_fg[:, :, scale_words - 1:scale_words], 0)
        nc.vector.memset(x_scales[:, PAD, :, :].bitcast(I32), 0)
        for g in range(GROUPS):
            dst = x_grouped[:, g, :].rearrange("p (l j) -> p l j", j=PACK)
            src = x_raw[:, g, :].rearrange("p (j l) -> p l j", j=PACK)
            if g == 0:
                nc.vector.tensor_copy(out=dst, in_=src)
            else:
                nc.scalar.copy(out=dst, in_=src)
        for g in range(GROUPS):
            nc.vector.quantize_mx(out=x_codes[:, PAD, g, :].bitcast(FP8X4), scales=x_scales[:, PAD, g, :],
                                  in_=x_grouped[:, g, :])
        for f in range(TAPS):
            d = f - PAD
            if d != 0:
                lo, hi = max(0, -d), L - max(0, d)
                nc.vector.tensor_copy(out=x_codes[:, f, :, lo:hi], in_=x_codes[:, PAD, :, lo + d:hi + d])

        def scale_plane(f):
            return x_scales[:, f, :, :].bitcast(I32)

        for d in (1, 2, 3):
            nc.vector.tensor_copy(out=x_scales[:, PAD + d, :, 0:L - d], in_=x_scales[:, PAD, :, d:L])
        nc.vector.tensor_copy(out=scale_plane(2 * PAD)[:, :, 0:scale_words - 1], in_=scale_plane(PAD)[:, :, 1:scale_words])
        nc.vector.tensor_copy(out=scale_plane(0)[:, :, 1:scale_words], in_=scale_plane(PAD)[:, :, 0:scale_words - 1])
        for d in (1, 2, 3):
            nc.vector.tensor_copy(out=scale_plane(d)[:, :, 1:scale_words], in_=scale_plane(PAD + d)[:, :, 0:scale_words - 1])
            nc.vector.tensor_copy(out=x_scales[:, d, :, PAD - d:PAD], in_=x_scales[:, PAD, :, 0:d])

        result_all = const.tile([P, GROUPS * L + 1], F32)
        result = result_all[:, 0:GROUPS * L].rearrange("p (g l) -> p g l", g=GROUPS)
        result8 = const.tile([P, GROUPS, L], FP8)
        peaks = const.tile([P, GROUPS], F32)
        grouped = {}
        accs = {}

        def interleave(index):
            g, c0, n, n_vector = DIRECT[index]
            if c0 == 0:
                big = big_pool.tile([P, SF * CO * PACK], BF16, tag="big", align_bytes=64)
                grouped[g] = big
            dst = grouped[g][:].rearrange("p (a b y) -> p a y b", a=SF // RUN, b=RUN)
            src = raws[index][:].rearrange("p c y -> p (c y)").rearrange("p (x a b) -> p a x b", a=SF // RUN, b=RUN)
            if n_vector > 0:
                nc.vector.tensor_copy(
                    out=dst[:, :, PACK * c0:PACK * (c0 + n_vector), :].rearrange("p a (h y) b -> p h a y b", h=2),
                    in_=src[:, :, 0:PACK * n_vector, :].rearrange("p a (h y) b -> p h a y b", h=2))
            if n_vector < n:
                nc.scalar.copy(out=dst[:, :, PACK * (c0 + n_vector):PACK * (c0 + n), :],
                               in_=src[:, :, PACK * n_vector:PACK * n, :])
            issue_loads_until(min(index + AHEAD, len(DIRECT) - 1))

        def turn(g, w):
            words = rows[g][:].bitcast(F32)
            bank = turn_psum.tile([P, PACK, CO], F32, tag="bank")
            step = PACK * WORDS
            for t in range(PACK):
                first = t * WORDS + w
                nc.tensor.transpose(bank[:, t, :], words[:, first:first + step * (P - 1) + 1:step], ident[:])
            return bank

        def empty(bank, part, i):
            dst = part[:, 2 * SF_IN * i:2 * SF_IN * (i + 1)].rearrange("p (e o t) -> p e o t", e=2, t=PACK)
            src = bank[:].rearrange("p t o -> p (t o)").bitcast(BF16).rearrange("p (t o e) -> p e o t", t=PACK, e=2)
            nc.scalar.copy(out=dst, in_=src)

        def quantize(g, sf0, n, values):
            codes = code_pool.tile([P, 8 * CO], I32, tag="codes", align_bytes=64)
            scales = code_pool.tile([P, 8 * CO], U8, tag="scales", align_bytes=64)
            nc.vector.quantize_mx(out=codes[:, 0:n * CO].bitcast(FP8X4), scales=scales[:, 0:n * CO], in_=values)
            return (g, sf0, n, codes, scales)

        def quantize_direct(g, call):
            sf0, n = call
            return quantize(g, sf0, n, grouped[g][:, SF_IN * sf0:SF_IN * (sf0 + n)])

        def finish_segment(g, s):
            base, start, end = SEG_BASE[s], SEG_START[s], SEG_END[s]
            nc.scalar.activation(out=result[:, g, start:end], in_=accs[g][:, s, start - base:end - base], func=ACT.Identity,
                                 bias=bias[:, 4 * g + s:4 * g + s + 1], scale=1.0)
            if s == 3:
                nc.scalar.dma_start(out=out0_view[g], in_=result[:, g, :])
            if g < 2 and s == 3:
                peak(g, L)

        def peak(g, end):
            nc.vector.tensor_reduce(out=peaks[:, g:g + 1], in_=result[:, g, 0:end], axis=AX.X, op=ALU.max,
                                    apply_absolute_value=True)

        def multiply(item):
            g, sf0, n, codes, scales = item
            closed = []
            if sf0 == 0:
                acc = acc_psum.tile([P, 4, P], F32, tag="acc")
                accs[g] = acc
            for i in range(n):
                s, f = divmod(sf0 + i, TAPS)
                base = SEG_BASE[s]
                nc.tensor.matmul_mx(
                    out=accs[g][:, s, :],
                    lhsT=codes[:, CO * i:CO * (i + 1)].bitcast(FP8X4), lhsT_scale=scales[:, CO * i:CO * (i + 1)],
                    rhs=x_codes[:, f, g, base:base + P].bitcast(FP8X4), rhs_scale=x_scales[:, f, g, base:base + P],
                    start=(f == 0), stop=(f == TAPS - 1),
                )
                if f == TAPS - 1:
                    closed.append((g, s))
            return closed

        def multiply_all(items):
            closed = []
            for i, item in enumerate(items):
                closed.extend(multiply(item))
                if i + 1 == len(items) or items[i + 1][0] != item[0]:
                    for g, s in closed:
                        finish_segment(g, s)
                    closed = []

        with tc.manual_schedule(engines={mybir.EngineType.PE}):
            interleave(0)
            chunk = 1
            waiting = []
            postponed = ()
            n_blocks = len(BANKS) // BLOCK
            for b in range(n_blocks):
                mine = BANKS[BLOCK * b:BLOCK * (b + 1)]
                banks = []
                for g, w in mine:
                    banks.append(turn(g, w))
                multiply_all(waiting)
                waiting = []
                for call in postponed:
                    waiting.append(quantize_direct(1, call))
                postponed = ()
                for i in range(CHUNKS_AFTER_BLOCK[b]):
                    interleave(chunk)
                    if chunk == GROUP1_LAST:
                        for call in WIDE_CALLS[:SPLIT]:
                            waiting.append(quantize_direct(1, call))
                        postponed = WIDE_CALLS[SPLIT:]
                    chunk += 1
                late = []
                for g in (0, 2):
                    some = [(w, bank) for (gg, w), bank in zip(mine, banks) if gg == g]
                    if len(some) > 0:
                        part = part_pool.tile([P, 8 * SF_IN], BF16, tag="part", align_bytes=64)
                        for i, (w, bank) in enumerate(some):
                            empty(bank, part, i)
                        unit = (g, 2 * some[0][0], 2 * len(some), part[:, 0:2 * len(some) * SF_IN])
                        if b < n_blocks - 1:
                            waiting.append(quantize(unit[0], unit[1], unit[2], unit[3]))
                        else:
                            late.append(unit)
            interleave(chunk)
            for i, call in enumerate(NARROW_CALLS):
                if i == 7:
                    for unit in late:
                        multiply_all([quantize(unit[0], unit[1], unit[2], unit[3])])
                multiply_all([quantize_direct(3, call)])

        peak(2, L)
        peak(3, SEG_START[3])
        copied = const.tile([P, GROUPS], F32)
        nc.vector.tensor_scalar(out=copied[:], in0=peaks[:], scalar1=1.0, scalar2=None, op0=ALU.mult, op1=ALU.max,
                                accum_out=result_all[:, GROUPS * L:GROUPS * L + 1])
        mine_max = const.tile([P, 1], F32)
        nc.vector.tensor_reduce(out=mine_max[:], in_=result_all[:, 3 * L + SEG_START[3]:GROUPS * L + 1], axis=AX.X, op=ALU.max,
                                apply_absolute_value=True)
        spread = turn_psum.tile([P, P], F32, tag="bank")
        nc.tensor.transpose(spread[:], mine_max[:, 0:1].to_broadcast([P, P]), ident[:])
        scale = const.tile([P, 1], F32)
        scaled = const.tile([P, P], F32)
        nc.vector.tensor_scalar(out=scaled[:], in0=spread[:], scalar1=1.0 / 448.0, scalar2=None, op0=ALU.mult, op1=ALU.max,
                                accum_out=scale[:])
        factor = const.tile([P, 1], F32)
        nc.vector.reciprocal(out=factor[:], in_=scale[:])
        nc.scalar.activation(out=result8[:, 3, :], in_=result[:, 3, :], func=ACT.Identity, scale=factor[:, 0:1],
                             bias=zero[:, 0:1], saturate=False)
        nc.vector.tensor_scalar(out=result8[:, 0:2, :], in0=result[:, 0:2, :], scalar1=factor[:, 0:1], scalar2=None,
                                op0=ALU.mult, saturate=False)
        nc.sync.dma_start(out=out1_view[:, 0:2, :], in_=result8[:, 0:2, :].bitcast(U8))
        nc.vector.tensor_scalar(out=result8[:, 2, :], in0=result[:, 2, :], scalar1=factor[:, 0:1], scalar2=None,
                                op0=ALU.mult, saturate=False)
        nc.sync.dma_start(out=out1_view[:, 2:4, :], in_=result8[:, 2:4, :].bitcast(U8))
